import numpy as np
import ml_dtypes


def mxq(x, axis, fmt="e4m3"):
    dtype, down = {"e4m3": (ml_dtypes.float8_e4m3fn, 7), "e5m2": (ml_dtypes.float8_e5m2, 14)}[fmt]
    v = np.moveaxis(np.asarray(x, np.float32).astype(ml_dtypes.bfloat16).astype(np.float64), axis, -1)
    blocks = v.reshape(v.shape[:-1] + (-1, 32))
    amax = np.abs(blocks).max(-1, keepdims=True)
    byte = np.maximum(np.where(amax > 0, np.frexp(amax)[1] - 1 + 127, 0) - down, 1)
    scale = np.exp2(byte - 127.0)
    codes = (blocks / scale).astype(np.float32).astype(dtype).astype(np.float64)
    return np.moveaxis((codes * scale).reshape(v.shape), -1, axis)


WIDE = False


def mx_kscale(k):
    if not WIDE:
        return np.ones(k)
    levels = np.array([10, -10, 5, -5, 0])
    a = np.random.permutation(np.resize(levels, k // 512 * 4)).reshape(k // 512, 4)
    idx = np.arange(k)
    return np.exp2(a[idx // 512, idx % 128 // 32])


BF16 = ml_dtypes.bfloat16


def bf(x):
    return np.asarray(x, np.float32).astype(BF16)


def f64(x):
    return np.asarray(x).astype(np.float64)


B, S, D, F, G, K = 2, 256, 512, 2048, 5, 3
N = B * S
NB = G + K
C = D * NB


def silu(v):
    e = np.exp(-np.abs(v))
    return v * np.where(v >= 0, 1.0, e) / (1.0 + e)


def b_splines(x, grid, k):
    x = x[..., None]
    bases = np.where((x >= grid[:-1]) & (x < grid[1:]), 1.0, 0.0)
    for j in range(1, k + 1):
        left = (x - grid[: -(j + 1)]) / (grid[j:-1] - grid[: -(j + 1)])
        right = (grid[j + 1:] - x) / (grid[j + 1:] - grid[1:-j])
        bases = left * bases[..., :-1] + right * bases[..., 1:]
    return bases


def setup_inputs():
    t = np.maximum(mx_kscale(D), 1.0) ** 2
    return {"x": bf(np.random.standard_normal((B, S, D)) * t),
            "grid": bf(np.arange(-K, G + K + 1) * (2.0 / G) - 1.0),
            "w1_base": bf(np.random.standard_normal((F, D)) / np.sqrt(D) / t),
            "w1_spline": bf(np.random.standard_normal((F, D, NB)) / np.sqrt(D))}


def reference(x, grid, w1_base, w1_spline):
    xf = f64(x).reshape(N, D)
    base = mxq(silu(xf), 1, "e4m3") @ mxq(f64(w1_base), 1, "e4m3").T
    bases = b_splines(xf, f64(grid), K).reshape(N, C)
    spline = mxq(bases, 1, "e4m3") @ mxq(f64(w1_spline).reshape(F, C), 1, "e4m3").T
    return base + spline

@@ -1,0 +1,283 @@
+from contextlib import ExitStack
+
+import concourse.mybir as mybir
+from concourse.masks import make_identity
+
+F32 = mybir.dt.float32
+BF16 = mybir.dt.bfloat16
+U32 = mybir.dt.uint32
+U8 = mybir.dt.uint8
+FP8X4 = mybir.dt.float8_e4m3fn_x4
+ALU = mybir.AluOpType
+ACT = mybir.ActivationFunctionType
+
+P = 128
+PACK = 4
+K_PASS = P * PACK
+TOKENS = 512
+D = 512
+F_OUT = 2048
+KNOTS = 12
+NB = 8
+K_ALL = D + D * NB
+PASSES = K_ALL // K_PASS
+TOKEN_TILES = TOKENS // P
+F_TILE = 512
+F_TILES = F_OUT // F_TILE
+ROWS_PER_F_TILE = F_TILE // P
+PAIRS = K_ALL // 2
+PASS_PAIRS = K_PASS // 2
+LOAD_PASSES = 2
+
+FLOPS = 2 * TOKENS * F_OUT * K_ALL
+
+
+def spline_constants(nc, const, grid):
+    knots_bf = const.tile([P, KNOTS], BF16)
+    nc.scalar.dma_start(out=knots_bf[:], in_=grid.partition_broadcast(P))
+    knots = const.tile([P, KNOTS], F32)
+    nc.vector.tensor_copy(out=knots[:], in_=knots_bf[:])
+    neg_knots = const.tile([P, KNOTS], F32)
+    nc.vector.tensor_scalar_mul(out=neg_knots[:], in0=knots[:], scalar1=-1.0)
+
+    gap1 = const.tile([P, KNOTS - 1], F32)
+    nc.vector.tensor_sub(out=gap1[:], in0=knots[:, 1:], in1=knots[:, : KNOTS - 1])
+    gap2 = const.tile([P, KNOTS - 2], F32)
+    nc.vector.tensor_sub(out=gap2[:], in0=knots[:, 2:], in1=knots[:, : KNOTS - 2])
+    gap3 = const.tile([P, KNOTS - 3], F32)
+    nc.vector.tensor_sub(out=gap3[:], in0=knots[:, 3:], in1=knots[:, : KNOTS - 3])
+    gap4 = const.tile([P, KNOTS - 4], F32)
+    nc.vector.tensor_sub(out=gap4[:], in0=knots[:, 4:], in1=knots[:, : KNOTS - 4])
+
+    n_cubes = KNOTS - 3
+    rise_den = const.tile([P, n_cubes], F32)
+    nc.vector.tensor_mul(out=rise_den[:], in0=gap1[:, :n_cubes], in1=gap2[:, :n_cubes])
+    nc.vector.tensor_mul(out=rise_den[:], in0=rise_den[:], in1=gap3[:])
+    rise_scale = const.tile([P, n_cubes], F32)
+    nc.vector.reciprocal(out=rise_scale[:], in_=rise_den[:])
+    fall_den = const.tile([P, n_cubes], F32)
+    nc.vector.tensor_mul(out=fall_den[:], in0=gap1[:, 2:], in1=gap2[:, 1:])
+    nc.vector.tensor_mul(out=fall_den[:], in0=fall_den[:], in1=gap3[:])
+    fall_scale = const.tile([P, n_cubes], F32)
+    nc.vector.reciprocal(out=fall_scale[:], in_=fall_den[:])
+    neg_fall_scale = const.tile([P, n_cubes], F32)
+    nc.vector.tensor_scalar_mul(out=neg_fall_scale[:], in0=fall_scale[:], scalar1=-1.0)
+
+    inv_gap1 = const.tile([P, KNOTS - 1], F32)
+    nc.vector.reciprocal(out=inv_gap1[:], in_=gap1[:])
+    neg_left_ratio = const.tile([P, NB], F32)
+    nc.vector.scalar_tensor_tensor(
+        out=neg_left_ratio[:], in0=gap4[:], scalar=-1.0, in1=inv_gap1[:, :NB],
+        op0=ALU.mult, op1=ALU.mult,
+    )
+    neg_right_ratio = const.tile([P, NB], F32)
+    nc.vector.scalar_tensor_tensor(
+        out=neg_right_ratio[:], in0=gap4[:], scalar=-1.0, in1=inv_gap1[:, 3:],
+        op0=ALU.mult, op1=ALU.mult,
+    )
+    return {
+        "knots": knots,
+        "neg_knots": neg_knots,
+        "rise_scale": rise_scale,
+        "neg_fall_scale": neg_fall_scale,
+        "neg_left_ratio": neg_left_ratio,
+        "neg_right_ratio": neg_right_ratio,
+    }
+
+
+def token_tile_activations(nc, planes, sides, acts_pool, consts, x_tile, x_clamped_tile):
+    knots = consts["knots"]
+    left = sides.tile([P, NB, D], BF16)
+    right = sides.tile([P, NB, D], BF16)
+    rise_prev = None
+    fall_prev = None
+    for j in range(KNOTS):
+        square = planes.tile([P, D], F32)
+        nc.scalar.activation(
+            out=square[:], in_=x_clamped_tile, func=ACT.Square,
+            bias=consts["neg_knots"][:, j : j + 1], scale=1.0,
+        )
+        cube = planes.tile([P, D], F32)
+        nc.vector.scalar_tensor_tensor(
+            out=cube[:], in0=x_clamped_tile, scalar=knots[:, j : j + 1], in1=square[:],
+            op0=ALU.subtract, op1=ALU.mult,
+        )
+        if j <= NB:
+            rise = planes.tile([P, D], F32)
+            nc.scalar.activation(
+                out=rise[:], in_=cube[:], func=ACT.Relu, scale=consts["rise_scale"][:, j : j + 1]
+            )
+            if j >= 1:
+                b = j - 1
+                nc.vector.scalar_tensor_tensor(
+                    out=left[:, b, :], in0=rise[:], scalar=consts["neg_left_ratio"][:, b : b + 1],
+                    in1=rise_prev[:], op0=ALU.mult, op1=ALU.add,
+                )
+            rise_prev = rise
+        if j >= 3:
+            fall = planes.tile([P, D], F32)
+            nc.vector.tensor_scalar(
+                out=fall[:], in0=cube[:], scalar1=0.0,
+                scalar2=consts["neg_fall_scale"][:, j - 3 : j - 2], op0=ALU.min, op1=ALU.mult,
+            )
+            if j >= 4:
+                b = j - 4
+                nc.vector.scalar_tensor_tensor(
+                    out=right[:, b, :], in0=fall_prev[:],
+                    scalar=consts["neg_right_ratio"][:, b : b + 1], in1=fall[:],
+                    op0=ALU.mult, op1=ALU.add,
+                )
+            fall_prev = fall
+
+    acts = acts_pool.tile([P, 2, PAIRS], BF16)
+    for e in range(2):
+        nc.vector.tensor_tensor(
+            out=acts[:, e, D // 2 :].rearrange("p (c i r) -> p c r i", i=4, r=NB // 2),
+            in0=left[:].rearrange("p (r e) (c i) -> p e c r i", e=2, i=4)[:, e],
+            in1=right[:].rearrange("p (r e) (c i) -> p e c r i", e=2, i=4)[:, e],
+            op=ALU.max,
+        )
+    nc.scalar.activation(
+        out=acts[:, :, : D // 2], in_=x_tile.rearrange("p (q e) -> p e q", e=2), func=ACT.Silu
+    )
+    return acts
+
+
+def activations_to_mx(nc, flips, stage, ident_bf, acts, codes, scales):
+    for g0 in range(0, PASSES, 2):
+        n_pass = min(2, PASSES - g0)
+        flipped = flips.tile([P, 2, PACK, P], BF16, tag="flip")
+        for g in range(n_pass):
+            for u in range(2):
+                for e in range(2):
+                    first = (g0 + g) * PASS_PAIRS + u * P
+                    nc.tensor.transpose(
+                        flipped[:, g, 2 * u + e, :], acts[:, e, first : first + P], ident_bf[:]
+                    )
+        grouped = stage.tile([P, 2, P, PACK], BF16, align_bytes=64, tag="a_grouped")
+        nc.scalar.copy(
+            out=grouped[:, :n_pass], in_=flipped[:, :n_pass].rearrange("p g t n -> p g n t")
+        )
+        nc.vector.quantize_mx(
+            out=codes[:, g0 : g0 + n_pass, :].rearrange("p g n -> p (g n)").bitcast(FP8X4),
+            scales=scales[:, g0 : g0 + n_pass, :].rearrange("p g n -> p (g n)"),
+            in_=grouped[:, :n_pass].rearrange("p g n t -> p (g n t)"),
+        )
+
+
+def weights_to_mx(nc, flips, stage, ident_f32, raw, n_pass, codes, scales):
+    words = raw.bitcast(F32)
+    for g in range(n_pass):
+        grouped = stage.tile([P, F_TILE, PACK], BF16, align_bytes=64, tag="w_grouped")
+        for half in range(2):
+            flipped = flips.tile([P, 2, 2 * P], F32, tag="flip")
+            for a in range(2):
+                for u in range(2):
+                    first = g * PASS_PAIRS + u * P
+                    nc.tensor.transpose(
+                        flipped[:, u, a * P : (a + 1) * P],
+                        words[:, 2 * half + a, first : first + P],
+                        ident_f32[:],
+                    )
+            nc.scalar.copy(
+                out=grouped[:, half * 2 * P : (half + 1) * 2 * P, :].bitcast(F32),
+                in_=flipped[:].rearrange("p u f -> p f u"),
+            )
+        nc.vector.quantize_mx(
+            out=codes[:, g, :].bitcast(FP8X4),
+            scales=scales[:, g, :],
+            in_=grouped[:].rearrange("p f t -> p (f t)"),
+        )
+
+
+def tile_kanblock_pa_kernel(tc, x, grid, w1_base, w1_spline, out):
+    nc = tc.nc
+    x_rows = x.rearrange("b s d -> (b s) d").rearrange("(t p) d -> p t d", p=P)
+    base_rows = w1_base.rearrange("(a p) k -> p a k", p=P)
+    spline_rows = w1_spline.rearrange("(a p) i b -> p a (i b)", p=P)
+
+    with ExitStack() as pools:
+        const = pools.enter_context(tc.tile_pool(name="const", bufs=1))
+        keep = pools.enter_context(tc.tile_pool(name="keep", bufs=1))
+        loads = pools.enter_context(tc.tile_pool(name="loads", bufs=3))
+        stage = pools.enter_context(tc.tile_pool(name="stage", bufs=2))
+        planes = pools.enter_context(tc.tile_pool(name="planes", bufs=3))
+        sides = pools.enter_context(tc.tile_pool(name="sides", bufs=1))
+        acts_pool = pools.enter_context(tc.tile_pool(name="acts", bufs=2))
+        results = pools.enter_context(tc.tile_pool(name="results", bufs=3))
+        flips = pools.enter_context(tc.psum_pool(name="flips", bufs=4))
+        sums = pools.enter_context(tc.psum_pool(name="sums", bufs=4))
+
+        x_sb = const.tile([P, TOKEN_TILES, D], BF16)
+        nc.sync.dma_start(out=x_sb[:], in_=x_rows)
+        consts = spline_constants(nc, const, grid)
+        ident_f32 = const.tile([P, P], F32)
+        make_identity(nc, ident_f32[:])
+        ident_bf = const.tile([P, P], BF16)
+        make_identity(nc, ident_bf[:])
+
+        x_clamped = const.tile([P, TOKEN_TILES, D], BF16)
+        nc.vector.tensor_scalar(
+            out=x_clamped[:], in0=x_sb[:], scalar1=consts["knots"][:, 0:1],
+            scalar2=consts["knots"][:, KNOTS - 1 : KNOTS], op0=ALU.max, op1=ALU.min,
+        )
+
+        a_codes = keep.tile([P, TOKEN_TILES, PASSES, P], U32, align_bytes=64)
+        a_scales = keep.tile([P, TOKEN_TILES, PASSES, P], U8, align_bytes=64)
+        w_codes = keep.tile([P, PASSES, F_OUT], U32, align_bytes=64)
+        w_scales = keep.tile([P, PASSES, F_OUT], U8, align_bytes=64)
+
+        def prepare_tokens(nt):
+            acts = token_tile_activations(
+                nc, planes, sides, acts_pool, consts, x_sb[:, nt, :], x_clamped[:, nt, :]
+            )
+            activations_to_mx(
+                nc, flips, stage, ident_bf, acts, a_codes[:, nt], a_scales[:, nt]
+            )
+
+        def prepare_weights(ft):
+            rows = slice(ft * ROWS_PER_F_TILE, (ft + 1) * ROWS_PER_F_TILE)
+            cols = slice(ft * F_TILE, (ft + 1) * F_TILE)
+            raw = loads.tile([P, ROWS_PER_F_TILE, LOAD_PASSES * K_PASS], BF16, tag="w_raw")
+            nc.sync.dma_start(out=raw[:, :, :K_PASS], in_=base_rows[:, rows, :])
+            weights_to_mx(
+                nc, flips, stage, ident_f32, raw[:, :, :K_PASS], 1,
+                w_codes[:, 0:1, cols], w_scales[:, 0:1, cols],
+            )
+            for g0 in range(1, PASSES, LOAD_PASSES):
+                raw = loads.tile([P, ROWS_PER_F_TILE, LOAD_PASSES * K_PASS], BF16, tag="w_raw")
+                first = (g0 - 1) * K_PASS
+                nc.sync.dma_start(
+                    out=raw[:], in_=spline_rows[:, rows, first : first + LOAD_PASSES * K_PASS]
+                )
+                weights_to_mx(
+                    nc, flips, stage, ident_f32, raw[:], LOAD_PASSES,
+                    w_codes[:, g0 : g0 + LOAD_PASSES, cols],
+                    w_scales[:, g0 : g0 + LOAD_PASSES, cols],
+                )
+
+        def multiply(nt):
+            for ft in range(F_TILES):
+                cols = slice(ft * F_TILE, (ft + 1) * F_TILE)
+                acc = sums.tile([P, F_TILE], F32)
+                for g in range(PASSES):
+                    nc.tensor.matmul_mx(
+                        out=acc[:],
+                        lhsT=a_codes[:, nt, g, :].bitcast(FP8X4),
+                        lhsT_scale=a_scales[:, nt, g, :],
+                        rhs=w_codes[:, g, cols].bitcast(FP8X4),
+                        rhs_scale=w_scales[:, g, cols],
+                        start=(g == 0),
+                        stop=(g == PASSES - 1),
+                    )
+                result = results.tile([P, F_TILE], F32)
+                nc.scalar.copy(out=result[:], in_=acc[:])
+                nc.sync.dma_start(out=out[nt * P : (nt + 1) * P, cols], in_=result[:])
+
+        prepare_tokens(0)
+        for ft in range(F_TILES):
+            prepare_weights(ft)
+        multiply(0)
+        for nt in range(1, TOKEN_TILES):
+            prepare_tokens(nt)
+            multiply(nt)

@@ -28,6 +28,10 @@ ROWS_PER_F_TILE = F_TILE // P
 PAIRS = K_ALL // 2
 PASS_PAIRS = K_PASS // 2
 LOAD_PASSES = 2
+SLICE_GAP = 2
+BANKS_FIRST = 4
+BANKS_SECOND = 2
+FEATURES_PER_PASS = K_PASS // NB
 
 FLOPS = 2 * TOKENS * F_OUT * K_ALL
 
@@ -85,116 +89,45 @@ def spline_constants(nc, const, grid):
     }
 
 
-def token_tile_activations(nc, planes, sides, acts_pool, consts, x_tile, x_clamped_tile):
-    knots = consts["knots"]
-    left = sides.tile([P, NB, D], BF16)
-    right = sides.tile([P, NB, D], BF16)
-    rise_prev = None
-    fall_prev = None
-    for j in range(KNOTS):
-        square = planes.tile([P, D], F32)
-        nc.scalar.activation(
-            out=square[:], in_=x_clamped_tile, func=ACT.Square,
-            bias=consts["neg_knots"][:, j : j + 1], scale=1.0,
-        )
-        cube = planes.tile([P, D], F32)
-        nc.vector.scalar_tensor_tensor(
-            out=cube[:], in0=x_clamped_tile, scalar=knots[:, j : j + 1], in1=square[:],
-            op0=ALU.subtract, op1=ALU.mult,
-        )
-        if j <= NB:
-            rise = planes.tile([P, D], F32)
-            nc.scalar.activation(
-                out=rise[:], in_=cube[:], func=ACT.Relu, scale=consts["rise_scale"][:, j : j + 1]
-            )
-            if j >= 1:
-                b = j - 1
-                nc.vector.scalar_tensor_tensor(
-                    out=left[:, b, :], in0=rise[:], scalar=consts["neg_left_ratio"][:, b : b + 1],
-                    in1=rise_prev[:], op0=ALU.mult, op1=ALU.add,
-                )
-            rise_prev = rise
-        if j >= 3:
-            fall = planes.tile([P, D], F32)
-            nc.vector.tensor_scalar(
-                out=fall[:], in0=cube[:], scalar1=0.0,
-                scalar2=consts["neg_fall_scale"][:, j - 3 : j - 2], op0=ALU.min, op1=ALU.mult,
-            )
-            if j >= 4:
-                b = j - 4
-                nc.vector.scalar_tensor_tensor(
-                    out=right[:, b, :], in0=fall_prev[:],
-                    scalar=consts["neg_right_ratio"][:, b : b + 1], in1=fall[:],
-                    op0=ALU.mult, op1=ALU.add,
-                )
-            fall_prev = fall
-
-    acts = acts_pool.tile([P, 2, PAIRS], BF16)
-    for e in range(2):
-        nc.vector.tensor_tensor(
-            out=acts[:, e, D // 2 :].rearrange("p (c i r) -> p c r i", i=4, r=NB // 2),
-            in0=left[:].rearrange("p (r e) (c i) -> p e c r i", e=2, i=4)[:, e],
-            in1=right[:].rearrange("p (r e) (c i) -> p e c r i", e=2, i=4)[:, e],
-            op=ALU.max,
-        )
-    nc.scalar.activation(
-        out=acts[:, :, : D // 2], in_=x_tile.rearrange("p (q e) -> p e q", e=2), func=ACT.Silu
-    )
-    return acts
-
-
-def activations_to_mx(nc, flips, stage, ident_bf, acts, codes, scales):
-    for g0 in range(0, PASSES, 2):
-        n_pass = min(2, PASSES - g0)
-        flipped = flips.tile([P, 2, PACK, P], BF16, tag="flip")
-        for g in range(n_pass):
-            for u in range(2):
-                for e in range(2):
-                    first = (g0 + g) * PASS_PAIRS + u * P
-                    nc.tensor.transpose(
-                        flipped[:, g, 2 * u + e, :], acts[:, e, first : first + P], ident_bf[:]
-                    )
-        grouped = stage.tile([P, 2, P, PACK], BF16, align_bytes=64, tag="a_grouped")
-        nc.scalar.copy(
-            out=grouped[:, :n_pass], in_=flipped[:, :n_pass].rearrange("p g t n -> p g n t")
-        )
-        nc.vector.quantize_mx(
-            out=codes[:, g0 : g0 + n_pass, :].rearrange("p g n -> p (g n)").bitcast(FP8X4),
-            scales=scales[:, g0 : g0 + n_pass, :].rearrange("p g n -> p (g n)"),
-            in_=grouped[:, :n_pass].rearrange("p g n t -> p (g n t)"),
-        )
-
-
-def weights_to_mx(nc, flips, stage, ident_f32, raw, n_pass, codes, scales):
-    words = raw.bitcast(F32)
-    for g in range(n_pass):
-        grouped = stage.tile([P, F_TILE, PACK], BF16, align_bytes=64, tag="w_grouped")
-        for half in range(2):
-            flipped = flips.tile([P, 2, 2 * P], F32, tag="flip")
-            for a in range(2):
-                for u in range(2):
-                    first = g * PASS_PAIRS + u * P
-                    nc.tensor.transpose(
-                        flipped[:, u, a * P : (a + 1) * P],
-                        words[:, 2 * half + a, first : first + P],
-                        ident_f32[:],
-                    )
-            nc.scalar.copy(
-                out=grouped[:, half * 2 * P : (half + 1) * 2 * P, :].bitcast(F32),
-                in_=flipped[:].rearrange("p u f -> p f u"),
-            )
-        nc.vector.quantize_mx(
-            out=codes[:, g, :].bitcast(FP8X4),
-            scales=scales[:, g, :],
-            in_=grouped[:].rearrange("p f t -> p (f t)"),
-        )
-
-
 def tile_kanblock_pa_kernel(tc, x, grid, w1_base, w1_spline, out):
     nc = tc.nc
     x_rows = x.rearrange("b s d -> (b s) d").rearrange("(t p) d -> p t d", p=P)
     base_rows = w1_base.rearrange("(a p) k -> p a k", p=P)
     spline_rows = w1_spline.rearrange("(a p) i b -> p a (i b)", p=P)
+
+    levels = [(0, 1)] + [(g, LOAD_PASSES) for g in range(1, PASSES, LOAD_PASSES)]
+
+    pieces = []
+    for nt in range(TOKEN_TILES):
+        cuts = 2 if nt == TOKEN_TILES - 1 else 1
+        for cut in range(cuts):
+            pieces.append((nt, cut * D // cuts, D // cuts))
+    n_steps = KNOTS * len(pieces)
+
+    banks = []
+    level_done = []
+    for first_pass, n_pass in levels:
+        for ft in range(F_TILES):
+            for g in range(first_pass, first_pass + n_pass):
+                for half in range(2):
+                    n = len(banks)
+                    if n < KNOTS * BANKS_FIRST:
+                        step = n // BANKS_FIRST
+                    else:
+                        step = KNOTS + (n - KNOTS * BANKS_FIRST) // BANKS_SECOND
+                    banks.append((step, ft, first_pass, n_pass, g, half))
+        level_done.append(banks[-1][0])
+
+    slices = []
+    free_step = 0
+    for piece, (nt, first_feature, n_features) in enumerate(pieces):
+        for level, (first_pass, n_pass) in enumerate(levels):
+            first_of_level = max(first_pass - 1, 0) * FEATURES_PER_PASS
+            if first_feature <= first_of_level < first_feature + n_features:
+                begin = max(free_step, KNOTS * (piece + 1) + 2, level_done[level] + 1)
+                slices.append((begin, nt, first_pass, n_pass))
+                free_step = begin + SLICE_GAP
+    last_step = slices[-1][0] + 4
 
     with ExitStack() as pools:
         const = pools.enter_context(tc.tile_pool(name="const", bufs=1))
@@ -204,9 +137,9 @@ def tile_kanblock_pa_kernel(tc, x, grid, w1_base, w1_spline, out):
         planes = pools.enter_context(tc.tile_pool(name="planes", bufs=3))
         sides = pools.enter_context(tc.tile_pool(name="sides", bufs=1))
         acts_pool = pools.enter_context(tc.tile_pool(name="acts", bufs=2))
-        results = pools.enter_context(tc.tile_pool(name="results", bufs=3))
+        results = pools.enter_context(tc.tile_pool(name="results", bufs=4))
         flips = pools.enter_context(tc.psum_pool(name="flips", bufs=4))
-        sums = pools.enter_context(tc.psum_pool(name="sums", bufs=4))
+        sums = pools.enter_context(tc.psum_pool(name="sums", bufs=1))
 
         x_sb = const.tile([P, TOKEN_TILES, D], BF16)
         nc.sync.dma_start(out=x_sb[:], in_=x_rows)
@@ -227,42 +160,173 @@ def tile_kanblock_pa_kernel(tc, x, grid, w1_base, w1_spline, out):
         w_codes = keep.tile([P, PASSES, F_OUT], U32, align_bytes=64)
         w_scales = keep.tile([P, PASSES, F_OUT], U8, align_bytes=64)
 
-        def prepare_tokens(nt):
-            acts = token_tile_activations(
-                nc, planes, sides, acts_pool, consts, x_sb[:, nt, :], x_clamped[:, nt, :]
+        live = {}
+
+        def piece_x(step):
+            nt, first_feature, n_features = pieces[step // KNOTS]
+            return x_clamped[:, nt, first_feature : first_feature + n_features], n_features
+
+        def square_stage(step):
+            xs, width = piece_x(step)
+            j = step % KNOTS
+            square = planes.tile([P, D], F32)
+            nc.scalar.activation(
+                out=square[:, :width], in_=xs, func=ACT.Square,
+                bias=consts["neg_knots"][:, j : j + 1], scale=1.0,
             )
-            activations_to_mx(
-                nc, flips, stage, ident_bf, acts, a_codes[:, nt], a_scales[:, nt]
+            live["square", step] = square
+
+        def cube_stage(step):
+            xs, width = piece_x(step)
+            j = step % KNOTS
+            cube = planes.tile([P, D], F32)
+            nc.vector.scalar_tensor_tensor(
+                out=cube[:, :width], in0=xs, scalar=consts["knots"][:, j : j + 1],
+                in1=live["square", step][:, :width], op0=ALU.subtract, op1=ALU.mult,
+            )
+            live["cube", step] = cube
+
+        def rise_stage(step):
+            width = piece_x(step)[1]
+            j = step % KNOTS
+            if j <= NB:
+                rise = planes.tile([P, D], F32, bufs=4)
+                nc.scalar.activation(
+                    out=rise[:, :width], in_=live["cube", step][:, :width], func=ACT.Relu,
+                    scale=consts["rise_scale"][:, j : j + 1],
+                )
+                live["rise", step] = rise
+
+        def fall_stage(step):
+            width = piece_x(step)[1]
+            j = step % KNOTS
+            if j >= 3:
+                fall = planes.tile([P, D], F32, bufs=4)
+                nc.vector.tensor_scalar(
+                    out=fall[:, :width], in0=live["cube", step][:, :width], scalar1=0.0,
+                    scalar2=consts["neg_fall_scale"][:, j - 3 : j - 2], op0=ALU.min, op1=ALU.mult,
+                )
+                live["fall", step] = fall
+
+        def left_stage(step):
+            width = piece_x(step)[1]
+            j = step % KNOTS
+            if j == 1:
+                live["left"] = sides.tile([P, NB, D], BF16, name="left")
+            if 1 <= j <= NB:
+                b = j - 1
+                nc.vector.scalar_tensor_tensor(
+                    out=live["left"][:, b, :width], in0=live["rise", step][:, :width],
+                    scalar=consts["neg_left_ratio"][:, b : b + 1],
+                    in1=live["rise", step - 1][:, :width], op0=ALU.mult, op1=ALU.add,
+                )
+
+        def right_stage(step):
+            width = piece_x(step)[1]
+            j = step % KNOTS
+            if j == 4:
+                live["right"] = sides.tile([P, NB, D], BF16, name="right")
+            if j >= 4:
+                b = j - 4
+                nc.vector.scalar_tensor_tensor(
+                    out=live["right"][:, b, :width], in0=live["fall", step - 1][:, :width],
+                    scalar=consts["neg_right_ratio"][:, b : b + 1],
+                    in1=live["fall", step][:, :width], op0=ALU.mult, op1=ALU.add,
+                )
+
+        def join_stage(piece, e):
+            nt, first_feature, width = pieces[piece]
+            if first_feature == 0 and e == 0:
+                live["acts", nt] = acts_pool.tile([P, 2, PAIRS], BF16, name="acts")
+                nc.scalar.activation(
+                    out=live["acts", nt][:, :, : D // 2],
+                    in_=x_sb[:, nt, :].rearrange("p (q e) -> p e q", e=2), func=ACT.Silu,
+                )
+            first_pair = D // 2 + first_feature * NB // 2
+            nc.vector.tensor_tensor(
+                out=live["acts", nt][:, e, first_pair : first_pair + width * NB // 2].rearrange(
+                    "p (c i r) -> p c r i", i=4, r=NB // 2
+                ),
+                in0=live["left"][:, :, :width].rearrange("p (r e) (c i) -> p e c r i", e=2, i=4)[
+                    :, e
+                ],
+                in1=live["right"][:, :, :width].rearrange("p (r e) (c i) -> p e c r i", e=2, i=4)[
+                    :, e
+                ],
+                op=ALU.max,
             )
 
-        def prepare_weights(ft):
+        def weight_bank_stage(ft, first_pass, n_pass, g, half):
             rows = slice(ft * ROWS_PER_F_TILE, (ft + 1) * ROWS_PER_F_TILE)
-            cols = slice(ft * F_TILE, (ft + 1) * F_TILE)
-            raw = loads.tile([P, ROWS_PER_F_TILE, LOAD_PASSES * K_PASS], BF16, tag="w_raw")
-            nc.sync.dma_start(out=raw[:, :, :K_PASS], in_=base_rows[:, rows, :])
-            weights_to_mx(
-                nc, flips, stage, ident_f32, raw[:, :, :K_PASS], 1,
-                w_codes[:, 0:1, cols], w_scales[:, 0:1, cols],
-            )
-            for g0 in range(1, PASSES, LOAD_PASSES):
+            if g == first_pass and half == 0:
                 raw = loads.tile([P, ROWS_PER_F_TILE, LOAD_PASSES * K_PASS], BF16, tag="w_raw")
-                first = (g0 - 1) * K_PASS
-                nc.sync.dma_start(
-                    out=raw[:], in_=spline_rows[:, rows, first : first + LOAD_PASSES * K_PASS]
+                if first_pass == 0:
+                    nc.sync.dma_start(out=raw[:, :, :K_PASS], in_=base_rows[:, rows, :])
+                else:
+                    first = (first_pass - 1) * K_PASS
+                    nc.sync.dma_start(
+                        out=raw[:], in_=spline_rows[:, rows, first : first + n_pass * K_PASS]
+                    )
+                live["w_words"] = raw[:].bitcast(F32)
+            if half == 0:
+                live["w_grouped", ft, g] = stage.tile(
+                    [P, F_TILE, PACK], BF16, align_bytes=64, name="w_grouped", bufs=3
                 )
-                weights_to_mx(
-                    nc, flips, stage, ident_f32, raw[:], LOAD_PASSES,
-                    w_codes[:, g0 : g0 + LOAD_PASSES, cols],
-                    w_scales[:, g0 : g0 + LOAD_PASSES, cols],
-                )
+            flipped = flips.tile([P, 2, 2 * P], F32, tag="flip")
+            for a in range(2):
+                for u in range(2):
+                    first = (g - first_pass) * PASS_PAIRS + u * P
+                    nc.tensor.transpose(
+                        flipped[:, u, a * P : (a + 1) * P],
+                        live["w_words"][:, 2 * half + a, first : first + P],
+                        ident_f32[:],
+                    )
+            nc.scalar.copy(
+                out=live["w_grouped", ft, g][:, half * 2 * P : (half + 1) * 2 * P, :].bitcast(F32),
+                in_=flipped[:].rearrange("p u f -> p f u"),
+            )
 
-        def multiply(nt):
+        def weight_quantise_stage(ft, g):
+            cols = slice(ft * F_TILE, (ft + 1) * F_TILE)
+            nc.vector.quantize_mx(
+                out=w_codes[:, g, cols].bitcast(FP8X4),
+                scales=w_scales[:, g, cols],
+                in_=live["w_grouped", ft, g][:].rearrange("p f t -> p (f t)"),
+            )
+
+        def flip_stage(nt, g0, n_pass):
+            acts = live["acts", nt]
+            flipped = flips.tile([P, LOAD_PASSES, PACK, P], BF16, tag="flip")
+            for g in range(n_pass):
+                for u in range(2):
+                    for e in range(2):
+                        first = (g0 + g) * PASS_PAIRS + u * P
+                        nc.tensor.transpose(
+                            flipped[:, g, 2 * u + e, :], acts[:, e, first : first + P], ident_bf[:]
+                        )
+            live["a_flipped", nt, g0] = flipped
+
+        def group_stage(nt, g0, n_pass):
+            grouped = stage.tile([P, LOAD_PASSES, P, PACK], BF16, align_bytes=64, name="a_grouped")
+            nc.scalar.copy(
+                out=grouped[:, :n_pass],
+                in_=live["a_flipped", nt, g0][:, :n_pass].rearrange("p g t n -> p g n t"),
+            )
+            live["a_grouped", nt, g0] = grouped
+
+        def multiply_stage(nt, g0, n_pass):
+            nc.vector.quantize_mx(
+                out=a_codes[:, nt, g0 : g0 + n_pass, :].rearrange("p g n -> p (g n)").bitcast(FP8X4),
+                scales=a_scales[:, nt, g0 : g0 + n_pass, :].rearrange("p g n -> p (g n)"),
+                in_=live["a_grouped", nt, g0][:, :n_pass].rearrange("p g n t -> p (g n t)"),
+            )
             for ft in range(F_TILES):
+                if g0 == 0:
+                    live["acc", ft] = sums.tile([P, F_TILE], F32, name="acc%d" % ft)
                 cols = slice(ft * F_TILE, (ft + 1) * F_TILE)
-                acc = sums.tile([P, F_TILE], F32)
-                for g in range(PASSES):
+                for g in range(g0, g0 + n_pass):
                     nc.tensor.matmul_mx(
-                        out=acc[:],
+                        out=live["acc", ft][:],
                         lhsT=a_codes[:, nt, g, :].bitcast(FP8X4),
                         lhsT_scale=a_scales[:, nt, g, :],
                         rhs=w_codes[:, g, cols].bitcast(FP8X4),
@@ -270,14 +334,43 @@ def tile_kanblock_pa_kernel(tc, x, grid, w1_base, w1_spline, out):
                         start=(g == 0),
                         stop=(g == PASSES - 1),
                     )
+
+        def store_stage(nt):
+            for ft in range(F_TILES):
+                cols = slice(ft * F_TILE, (ft + 1) * F_TILE)
                 result = results.tile([P, F_TILE], F32)
-                nc.scalar.copy(out=result[:], in_=acc[:])
+                if ft % 2 == 0 or nt < TOKEN_TILES - 1:
+                    nc.scalar.copy(out=result[:], in_=live["acc", ft][:])
+                else:
+                    nc.vector.tensor_copy(out=result[:], in_=live["acc", ft][:])
                 nc.sync.dma_start(out=out[nt * P : (nt + 1) * P, cols], in_=result[:])
 
-        prepare_tokens(0)
-        for ft in range(F_TILES):
-            prepare_weights(ft)
-        multiply(0)
-        for nt in range(1, TOKEN_TILES):
-            prepare_tokens(nt)
-            multiply(nt)
+        square_stage(0)
+        for step in range(last_step + 1):
+            if step + 1 < n_steps:
+                square_stage(step + 1)
+            if step < n_steps:
+                cube_stage(step)
+            for begin, nt, g0, n_pass in slices:
+                if begin == step:
+                    flip_stage(nt, g0, n_pass)
+                if begin == step - 1:
+                    group_stage(nt, g0, n_pass)
+            for bank_step, ft, first_pass, n_pass, g, half in banks:
+                if bank_step == step:
+                    weight_bank_stage(ft, first_pass, n_pass, g, half)
+                if bank_step == step - 1 and half == 1:
+                    weight_quantise_stage(ft, g)
+            for begin, nt, g0, n_pass in slices:
+                if begin == step - 2:
+                    multiply_stage(nt, g0, n_pass)
+                if begin == step - 4 and g0 + n_pass == PASSES:
+                    store_stage(nt)
+            if 1 <= step <= n_steps:
+                left_stage(step - 1)
+                right_stage(step - 1)
+            if KNOTS <= step <= n_steps + 1 and step % KNOTS < 2:
+                join_stage(step // KNOTS - 1, step % KNOTS)
+            if step < n_steps:
+                rise_stage(step)
+                fall_stage(step)

@@ -29,6 +29,7 @@ PAIRS = K_ALL // 2
 PASS_PAIRS = K_PASS // 2
 LOAD_PASSES = 2
 SLICE_GAP = 2
+RISE_SHARE = 3
 BANKS_FIRST = 4
 BANKS_SECOND = 2
 FEATURES_PER_PASS = K_PASS // NB
@@ -124,7 +125,7 @@ def tile_kanblock_pa_kernel(tc, x, grid, w1_base, w1_spline, out):
         for level, (first_pass, n_pass) in enumerate(levels):
             first_of_level = max(first_pass - 1, 0) * FEATURES_PER_PASS
             if first_feature <= first_of_level < first_feature + n_features:
-                begin = max(free_step, KNOTS * (piece + 1) + 2, level_done[level] + 1)
+                begin = max(free_step, KNOTS * (piece + 1) + 1, level_done[level] + 1)
                 slices.append((begin, nt, first_pass, n_pass))
                 free_step = begin + SLICE_GAP
     last_step = slices[-1][0] + 4
@@ -136,7 +137,7 @@ def tile_kanblock_pa_kernel(tc, x, grid, w1_base, w1_spline, out):
         stage = pools.enter_context(tc.tile_pool(name="stage", bufs=2))
         planes = pools.enter_context(tc.tile_pool(name="planes", bufs=3))
         sides = pools.enter_context(tc.tile_pool(name="sides", bufs=1))
-        acts_pool = pools.enter_context(tc.tile_pool(name="acts", bufs=2))
+        acts_pool = pools.enter_context(tc.tile_pool(name="acts", bufs=3))
         results = pools.enter_context(tc.tile_pool(name="results", bufs=4))
         flips = pools.enter_context(tc.psum_pool(name="flips", bufs=4))
         sums = pools.enter_context(tc.psum_pool(name="sums", bufs=1))
@@ -191,10 +192,16 @@ def tile_kanblock_pa_kernel(tc, x, grid, w1_base, w1_spline, out):
             j = step % KNOTS
             if j <= NB:
                 rise = planes.tile([P, D], F32, bufs=4)
-                nc.scalar.activation(
-                    out=rise[:, :width], in_=live["cube", step][:, :width], func=ACT.Relu,
-                    scale=consts["rise_scale"][:, j : j + 1],
-                )
+                if j % RISE_SHARE == 0:
+                    nc.vector.tensor_scalar(
+                        out=rise[:, :width], in0=live["cube", step][:, :width], scalar1=0.0,
+                        scalar2=consts["rise_scale"][:, j : j + 1], op0=ALU.max, op1=ALU.mult,
+                    )
+                else:
+                    nc.scalar.activation(
+                        out=rise[:, :width], in_=live["cube", step][:, :width], func=ACT.Relu,
+                        scale=consts["rise_scale"][:, j : j + 1],
+                    )
                 live["rise", step] = rise
 
         def fall_stage(step):
@@ -209,14 +216,15 @@ def tile_kanblock_pa_kernel(tc, x, grid, w1_base, w1_spline, out):
                 live["fall", step] = fall
 
         def left_stage(step):
-            width = piece_x(step)[1]
+            nt, first_feature, width = pieces[step // KNOTS]
             j = step % KNOTS
-            if j == 1:
-                live["left"] = sides.tile([P, NB, D], BF16, name="left")
+            if j == 1 and first_feature == 0:
+                live["bases", nt] = acts_pool.tile([P, NB, D], BF16, name="bases")
             if 1 <= j <= NB:
                 b = j - 1
                 nc.vector.scalar_tensor_tensor(
-                    out=live["left"][:, b, :width], in0=live["rise", step][:, :width],
+                    out=live["bases", nt][:, b, first_feature : first_feature + width],
+                    in0=live["rise", step][:, :width],
                     scalar=consts["neg_left_ratio"][:, b : b + 1],
                     in1=live["rise", step - 1][:, :width], op0=ALU.mult, op1=ALU.add,
                 )
@@ -234,27 +242,20 @@ def tile_kanblock_pa_kernel(tc, x, grid, w1_base, w1_spline, out):
                     in1=live["fall", step][:, :width], op0=ALU.mult, op1=ALU.add,
                 )
 
-        def join_stage(piece, e):
-            nt, first_feature, width = pieces[piece]
-            if first_feature == 0 and e == 0:
-                live["acts", nt] = acts_pool.tile([P, 2, PAIRS], BF16, name="acts")
-                nc.scalar.activation(
-                    out=live["acts", nt][:, :, : D // 2],
-                    in_=x_sb[:, nt, :].rearrange("p (q e) -> p e q", e=2), func=ACT.Silu,
-                )
-            first_pair = D // 2 + first_feature * NB // 2
-            nc.vector.tensor_tensor(
-                out=live["acts", nt][:, e, first_pair : first_pair + width * NB // 2].rearrange(
-                    "p (c i r) -> p c r i", i=4, r=NB // 2
-                ),
-                in0=live["left"][:, :, :width].rearrange("p (r e) (c i) -> p e c r i", e=2, i=4)[
-                    :, e
-                ],
-                in1=live["right"][:, :, :width].rearrange("p (r e) (c i) -> p e c r i", e=2, i=4)[
-                    :, e
-                ],
-                op=ALU.max,
+        def silu_stage(nt):
+            silu = acts_pool.tile([P, 2, D // 2], BF16)
+            nc.scalar.activation(
+                out=silu[:], in_=x_sb[:, nt, :].rearrange("p (q e) -> p e q", e=2), func=ACT.Silu
             )
+            live["silu", nt] = silu
+
+        def join_stage(piece):
+            nt, first_feature, width = pieces[piece]
+            for first in range(0, width, P):
+                block = live["bases", nt][:, :, first_feature + first : first_feature + first + P]
+                nc.vector.tensor_tensor(
+                    out=block, in0=block, in1=live["right"][:, :, first : first + P], op=ALU.max
+                )
 
         def weight_bank_stage(ft, first_pass, n_pass, g, half):
             rows = slice(ft * ROWS_PER_F_TILE, (ft + 1) * ROWS_PER_F_TILE)
@@ -275,10 +276,13 @@ def tile_kanblock_pa_kernel(tc, x, grid, w1_base, w1_spline, out):
             flipped = flips.tile([P, 2, 2 * P], F32, tag="flip")
             for a in range(2):
                 for u in range(2):
-                    first = (g - first_pass) * PASS_PAIRS + u * P
+                    if first_pass == 0:
+                        words = slice(u * P, (u + 1) * P)
+                    else:
+                        words = slice(2 * (g - first_pass) + u, PACK * P, PACK)
                     nc.tensor.transpose(
                         flipped[:, u, a * P : (a + 1) * P],
-                        live["w_words"][:, 2 * half + a, first : first + P],
+                        live["w_words"][:, 2 * half + a, words],
                         ident_f32[:],
                     )
             nc.scalar.copy(
@@ -295,15 +299,15 @@ def tile_kanblock_pa_kernel(tc, x, grid, w1_base, w1_spline, out):
             )
 
         def flip_stage(nt, g0, n_pass):
-            acts = live["acts", nt]
             flipped = flips.tile([P, LOAD_PASSES, PACK, P], BF16, tag="flip")
             for g in range(n_pass):
-                for u in range(2):
-                    for e in range(2):
-                        first = (g0 + g) * PASS_PAIRS + u * P
-                        nc.tensor.transpose(
-                            flipped[:, g, 2 * u + e, :], acts[:, e, first : first + P], ident_bf[:]
-                        )
+                for t in range(PACK):
+                    if g0 == 0:
+                        source = live["silu", nt][:, t % 2, (t // 2) * P : (t // 2 + 1) * P]
+                    else:
+                        first = (g0 - 1) // LOAD_PASSES * P
+                        source = live["bases", nt][:, PACK * g + t, first : first + P]
+                    nc.tensor.transpose(flipped[:, g, t, :], source, ident_bf[:])
             live["a_flipped", nt, g0] = flipped
 
         def group_stage(nt, g0, n_pass):
@@ -351,6 +355,8 @@ def tile_kanblock_pa_kernel(tc, x, grid, w1_base, w1_spline, out):
                 square_stage(step + 1)
             if step < n_steps:
                 cube_stage(step)
+                if step % KNOTS == 0 and pieces[step // KNOTS][1] == 0:
+                    silu_stage(pieces[step // KNOTS][0])
             for begin, nt, g0, n_pass in slices:
                 if begin == step:
                     flip_stage(nt, g0, n_pass)
@@ -369,8 +375,8 @@ def tile_kanblock_pa_kernel(tc, x, grid, w1_base, w1_spline, out):
             if 1 <= step <= n_steps:
                 left_stage(step - 1)
                 right_stage(step - 1)
-            if KNOTS <= step <= n_steps + 1 and step % KNOTS < 2:
-                join_stage(step // KNOTS - 1, step % KNOTS)
+            if KNOTS <= step <= n_steps and step % KNOTS == 0:
+                join_stage(step // KNOTS - 1)
             if step < n_steps:
                 rise_stage(step)
                 fall_stage(step)

@@ -29,7 +29,7 @@ PAIRS = K_ALL // 2
 PASS_PAIRS = K_PASS // 2
 LOAD_PASSES = 2
 SLICE_GAP = 2
-RISE_SHARE = 3
+RISE_SHARE = 1
 BANKS_FIRST = 4
 BANKS_SECOND = 2
 FEATURES_PER_PASS = K_PASS // NB

@@ -19,32 +19,31 @@ D = 512
 F_OUT = 2048
 KNOTS = 12
 NB = 8
+PAIRS = NB // 2
 K_ALL = D + D * NB
 PASSES = K_ALL // K_PASS
 TOKEN_TILES = TOKENS // P
 F_TILE = 512
 F_TILES = F_OUT // F_TILE
 ROWS_PER_F_TILE = F_TILE // P
-PAIRS = K_ALL // 2
-PASS_PAIRS = K_PASS // 2
-LOAD_PASSES = 2
-SLICE_GAP = 2
-RISE_SHARE = 1
-BANKS_FIRST = 4
-BANKS_SECOND = 2
-FEATURES_PER_PASS = K_PASS // NB
+ROWS_PER_BANK = 2
+HALF = D // 2
 
+BANKS_PER_STEP = 2
 FLOPS = 2 * TOKENS * F_OUT * K_ALL
 
 
-def spline_constants(nc, const, grid):
+def spline_knots(nc, const, grid):
     knots_bf = const.tile([P, KNOTS], BF16)
     nc.scalar.dma_start(out=knots_bf[:], in_=grid.partition_broadcast(P))
     knots = const.tile([P, KNOTS], F32)
     nc.vector.tensor_copy(out=knots[:], in_=knots_bf[:])
     neg_knots = const.tile([P, KNOTS], F32)
     nc.vector.tensor_scalar_mul(out=neg_knots[:], in0=knots[:], scalar1=-1.0)
+    return knots, neg_knots
 
+
+def spline_factors(nc, const, knots):
     gap1 = const.tile([P, KNOTS - 1], F32)
     nc.vector.tensor_sub(out=gap1[:], in0=knots[:, 1:], in1=knots[:, : KNOTS - 1])
     gap2 = const.tile([P, KNOTS - 2], F32)
@@ -58,36 +57,25 @@ def spline_constants(nc, const, grid):
     rise_den = const.tile([P, n_cubes], F32)
     nc.vector.tensor_mul(out=rise_den[:], in0=gap1[:, :n_cubes], in1=gap2[:, :n_cubes])
     nc.vector.tensor_mul(out=rise_den[:], in0=rise_den[:], in1=gap3[:])
-    rise_scale = const.tile([P, n_cubes], F32)
-    nc.vector.reciprocal(out=rise_scale[:], in_=rise_den[:])
+    rise = const.tile([P, n_cubes], F32)
+    nc.vector.reciprocal(out=rise[:], in_=rise_den[:])
     fall_den = const.tile([P, n_cubes], F32)
     nc.vector.tensor_mul(out=fall_den[:], in0=gap1[:, 2:], in1=gap2[:, 1:])
-    nc.vector.tensor_mul(out=fall_den[:], in0=fall_den[:], in1=gap3[:])
-    fall_scale = const.tile([P, n_cubes], F32)
-    nc.vector.reciprocal(out=fall_scale[:], in_=fall_den[:])
-    neg_fall_scale = const.tile([P, n_cubes], F32)
-    nc.vector.tensor_scalar_mul(out=neg_fall_scale[:], in0=fall_scale[:], scalar1=-1.0)
+    nc.vector.scalar_tensor_tensor(
+        out=fall_den[:], in0=fall_den[:], scalar=-1.0, in1=gap3[:], op0=ALU.mult, op1=ALU.mult
+    )
+    neg_fall = const.tile([P, n_cubes], F32)
+    nc.vector.reciprocal(out=neg_fall[:], in_=fall_den[:])
 
     inv_gap1 = const.tile([P, KNOTS - 1], F32)
     nc.vector.reciprocal(out=inv_gap1[:], in_=gap1[:])
-    neg_left_ratio = const.tile([P, NB], F32)
-    nc.vector.scalar_tensor_tensor(
-        out=neg_left_ratio[:], in0=gap4[:], scalar=-1.0, in1=inv_gap1[:, :NB],
-        op0=ALU.mult, op1=ALU.mult,
-    )
-    neg_right_ratio = const.tile([P, NB], F32)
-    nc.vector.scalar_tensor_tensor(
-        out=neg_right_ratio[:], in0=gap4[:], scalar=-1.0, in1=inv_gap1[:, 3:],
-        op0=ALU.mult, op1=ALU.mult,
-    )
-    return {
-        "knots": knots,
-        "neg_knots": neg_knots,
-        "rise_scale": rise_scale,
-        "neg_fall_scale": neg_fall_scale,
-        "neg_left_ratio": neg_left_ratio,
-        "neg_right_ratio": neg_right_ratio,
-    }
+    rise_inner = const.tile([P, NB], F32)
+    nc.vector.tensor_mul(out=rise_inner[:], in0=gap4[:], in1=inv_gap1[:, :NB])
+    nc.vector.tensor_mul(out=rise_inner[:], in0=rise_inner[:], in1=rise[:, 1:])
+    neg_fall_inner = const.tile([P, NB], F32)
+    nc.vector.tensor_mul(out=neg_fall_inner[:], in0=gap4[:], in1=inv_gap1[:, 3:])
+    nc.vector.tensor_mul(out=neg_fall_inner[:], in0=neg_fall_inner[:], in1=neg_fall[:, :NB])
+    return rise, rise_inner, neg_fall, neg_fall_inner
 
 
 def tile_kanblock_pa_kernel(tc, x, grid, w1_base, w1_spline, out):
@@ -96,66 +84,58 @@ def tile_kanblock_pa_kernel(tc, x, grid, w1_base, w1_spline, out):
     base_rows = w1_base.rearrange("(a p) k -> p a k", p=P)
     spline_rows = w1_spline.rearrange("(a p) i b -> p a (i b)", p=P)
 
-    levels = [(0, 1)] + [(g, LOAD_PASSES) for g in range(1, PASSES, LOAD_PASSES)]
-
-    pieces = []
-    for nt in range(TOKEN_TILES):
-        cuts = 2 if nt == TOKEN_TILES - 1 else 1
-        for cut in range(cuts):
-            pieces.append((nt, cut * D // cuts, D // cuts))
-    n_steps = KNOTS * len(pieces)
+    width = PACK * P
+    n_steps = KNOTS * TOKEN_TILES
 
     banks = []
-    level_done = []
-    for first_pass, n_pass in levels:
-        for ft in range(F_TILES):
-            for g in range(first_pass, first_pass + n_pass):
+    for ft in range(F_TILES):
+        for half in range(2):
+            banks.append(("base", ft, half, 0, 0))
+        for h in range(2):
+            for m in range(PAIRS):
                 for half in range(2):
-                    n = len(banks)
-                    if n < KNOTS * BANKS_FIRST:
-                        step = n // BANKS_FIRST
-                    else:
-                        step = KNOTS + (n - KNOTS * BANKS_FIRST) // BANKS_SECOND
-                    banks.append((step, ft, first_pass, n_pass, g, half))
-        level_done.append(banks[-1][0])
+                    banks.append(("spline", ft, half, h, m))
+    weights_done = [
+        ((ft + 1) * len(banks) // F_TILES - 1) // BANKS_PER_STEP + 1 for ft in range(F_TILES)
+    ]
 
-    slices = []
+    last_tile = TOKEN_TILES - 1
+    ready = []
+    for nt in range(last_tile):
+        for ft in range(F_TILES):
+            made = KNOTS * nt + 2 * PAIRS + 6
+            ready.append((max(made, weights_done[ft]) + 1, nt, -1, PAIRS - 1, (ft, ft + 1)))
+    for m in range(-1, PAIRS):
+        made = KNOTS * last_tile + (2 if m < 0 else 2 * m + 8)
+        ready.append((max(made, KNOTS * last_tile + 8) + 1, last_tile, m, m, (0, F_TILES)))
+    products = []
     free_step = 0
-    for piece, (nt, first_feature, n_features) in enumerate(pieces):
-        for level, (first_pass, n_pass) in enumerate(levels):
-            first_of_level = max(first_pass - 1, 0) * FEATURES_PER_PASS
-            if first_feature <= first_of_level < first_feature + n_features:
-                begin = max(free_step, KNOTS * (piece + 1) + 1, level_done[level] + 1)
-                slices.append((begin, nt, first_pass, n_pass))
-                free_step = begin + SLICE_GAP
-    last_step = slices[-1][0] + 4
+    for begin, nt, m0, m1, fts in sorted(ready):
+        begin = max(begin, free_step)
+        products.append((begin, nt, m0, m1, fts))
+        free_step = begin + 1
+    last_step = products[-1][0] + 1
 
     with ExitStack() as pools:
         const = pools.enter_context(tc.tile_pool(name="const", bufs=1))
         keep = pools.enter_context(tc.tile_pool(name="keep", bufs=1))
-        loads = pools.enter_context(tc.tile_pool(name="loads", bufs=3))
-        stage = pools.enter_context(tc.tile_pool(name="stage", bufs=2))
-        planes = pools.enter_context(tc.tile_pool(name="planes", bufs=3))
-        sides = pools.enter_context(tc.tile_pool(name="sides", bufs=1))
-        acts_pool = pools.enter_context(tc.tile_pool(name="acts", bufs=3))
+        loads = pools.enter_context(tc.tile_pool(name="loads", bufs=4))
+        stage = pools.enter_context(tc.tile_pool(name="stage", bufs=3))
+        planes = pools.enter_context(tc.tile_pool(name="planes", bufs=4))
         results = pools.enter_context(tc.tile_pool(name="results", bufs=4))
         flips = pools.enter_context(tc.psum_pool(name="flips", bufs=4))
-        sums = pools.enter_context(tc.psum_pool(name="sums", bufs=1))
+        sums = pools.enter_context(tc.psum_pool(name="sums", bufs=4))
 
         x_sb = const.tile([P, TOKEN_TILES, D], BF16)
-        nc.sync.dma_start(out=x_sb[:], in_=x_rows)
-        consts = spline_constants(nc, const, grid)
+        for nt in range(TOKEN_TILES):
+            nc.sync.dma_start(out=x_sb[:, nt, :], in_=x_rows[:, nt, :])
+        knots, neg_knots = spline_knots(nc, const, grid)
         ident_f32 = const.tile([P, P], F32)
         make_identity(nc, ident_f32[:])
         ident_bf = const.tile([P, P], BF16)
         make_identity(nc, ident_bf[:])
 
-        x_clamped = const.tile([P, TOKEN_TILES, D], BF16)
-        nc.vector.tensor_scalar(
-            out=x_clamped[:], in0=x_sb[:], scalar1=consts["knots"][:, 0:1],
-            scalar2=consts["knots"][:, KNOTS - 1 : KNOTS], op0=ALU.max, op1=ALU.min,
-        )
-
+        x_t = const.tile([P, TOKEN_TILES, 2, P, 2], BF16)
         a_codes = keep.tile([P, TOKEN_TILES, PASSES, P], U32, align_bytes=64)
         a_scales = keep.tile([P, TOKEN_TILES, PASSES, P], U8, align_bytes=64)
         w_codes = keep.tile([P, PASSES, F_OUT], U32, align_bytes=64)
@@ -163,130 +143,142 @@ def tile_kanblock_pa_kernel(tc, x, grid, w1_base, w1_spline, out):
 
         live = {}
 
-        def piece_x(step):
-            nt, first_feature, n_features = pieces[step // KNOTS]
-            return x_clamped[:, nt, first_feature : first_feature + n_features], n_features
+        def turn_stage(nt):
+            turned = flips.tile([P, PACK, P], BF16, tag="flip")
+            for c in range(PACK):
+                nc.tensor.transpose(turned[:, c, :], x_sb[:, nt, c * P : (c + 1) * P], ident_bf[:])
+            nc.vector.tensor_scalar(
+                out=x_t[:, nt], in0=turned[:].rearrange("p (h u) n -> p h n u", u=2),
+                scalar1=knots[:, 0:1], scalar2=knots[:, KNOTS - 1 : KNOTS],
+                op0=ALU.max, op1=ALU.min,
+            )
+
+        def silu_stage(nt):
+            words = x_sb[:, nt, :].bitcast(F32)
+            turned = flips.tile([P, 2, P], F32, tag="flip")
+            for u in range(2):
+                nc.tensor.transpose(turned[:, u, :], words[:, u * P : (u + 1) * P], ident_f32[:])
+            silu = stage.tile([P, P, PACK], BF16, align_bytes=64, name="silu", bufs=2)
+            nc.scalar.activation(
+                out=silu[:].rearrange("p n (u e) -> p n u e", u=2),
+                in_=turned[:].bitcast(BF16).rearrange("p u (n e) -> p n u e", e=2),
+                func=ACT.Silu,
+            )
+            live["silu", nt] = silu
+
+        def silu_quantise_stage(nt):
+            nc.vector.quantize_mx(
+                out=a_codes[:, nt, 0, :].bitcast(FP8X4),
+                scales=a_scales[:, nt, 0, :],
+                in_=live["silu", nt][:].rearrange("p n t -> p (n t)"),
+            )
+
+        def tile_x(step):
+            return x_t[:, step // KNOTS].rearrange("p h n u -> p (h n u)")
 
         def square_stage(step):
-            xs, width = piece_x(step)
             j = step % KNOTS
-            square = planes.tile([P, D], F32)
+            square = planes.tile([P, width], F32)
             nc.scalar.activation(
-                out=square[:, :width], in_=xs, func=ACT.Square,
-                bias=consts["neg_knots"][:, j : j + 1], scale=1.0,
+                out=square[:], in_=tile_x(step), func=ACT.Square,
+                bias=neg_knots[:, j : j + 1], scale=1.0,
             )
             live["square", step] = square
 
         def cube_stage(step):
-            xs, width = piece_x(step)
             j = step % KNOTS
-            cube = planes.tile([P, D], F32)
+            cube = planes.tile([P, width], F32)
             nc.vector.scalar_tensor_tensor(
-                out=cube[:, :width], in0=xs, scalar=consts["knots"][:, j : j + 1],
-                in1=live["square", step][:, :width], op0=ALU.subtract, op1=ALU.mult,
+                out=cube[:], in0=tile_x(step), scalar=knots[:, j : j + 1],
+                in1=live["square", step][:], op0=ALU.subtract, op1=ALU.mult,
             )
             live["cube", step] = cube
 
-        def rise_stage(step):
-            width = piece_x(step)[1]
+        def inner_stage(step):
             j = step % KNOTS
-            if j <= NB:
-                rise = planes.tile([P, D], F32, bufs=4)
-                if j % RISE_SHARE == 0:
-                    nc.vector.tensor_scalar(
-                        out=rise[:, :width], in0=live["cube", step][:, :width], scalar1=0.0,
-                        scalar2=consts["rise_scale"][:, j : j + 1], op0=ALU.max, op1=ALU.mult,
-                    )
-                else:
-                    nc.scalar.activation(
-                        out=rise[:, :width], in_=live["cube", step][:, :width], func=ACT.Relu,
-                        scale=consts["rise_scale"][:, j : j + 1],
-                    )
-                live["rise", step] = rise
+            cube = live["cube", step]
+            if 1 <= j <= NB:
+                above = planes.tile([P, width], F32)
+                factor = rise_inner[:, j - 1 : j]
+                nc.scalar.activation(out=above[:], in_=cube[:], func=ACT.Relu, scale=factor)
+                live["above", step] = above
+            if 3 <= j <= NB + 2:
+                below = planes.tile([P, width], F32)
+                factor = neg_fall_inner[:, j - 3 : j - 2]
+                nc.scalar.activation(out=below[:], in_=cube[:], func=ACT.Relu, scale=factor)
+                live["below", step] = below
 
-        def fall_stage(step):
-            width = piece_x(step)[1]
-            j = step % KNOTS
-            if j >= 3:
-                fall = planes.tile([P, D], F32, bufs=4)
-                nc.vector.tensor_scalar(
-                    out=fall[:, :width], in0=live["cube", step][:, :width], scalar1=0.0,
-                    scalar2=consts["neg_fall_scale"][:, j - 3 : j - 2], op0=ALU.min, op1=ALU.mult,
-                )
-                live["fall", step] = fall
-
-        def left_stage(step):
-            nt, first_feature, width = pieces[step // KNOTS]
-            j = step % KNOTS
-            if j == 1 and first_feature == 0:
-                live["bases", nt] = acts_pool.tile([P, NB, D], BF16, name="bases")
+        def side_stage(step):
+            nt, j = divmod(step, KNOTS)
             if 1 <= j <= NB:
                 b = j - 1
+                if b % 2 == 0:
+                    left = planes.tile([P, 2, width], BF16)
+                    live["left", nt, b // 2] = left
                 nc.vector.scalar_tensor_tensor(
-                    out=live["bases", nt][:, b, first_feature : first_feature + width],
-                    in0=live["rise", step][:, :width],
-                    scalar=consts["neg_left_ratio"][:, b : b + 1],
-                    in1=live["rise", step - 1][:, :width], op0=ALU.mult, op1=ALU.add,
+                    out=live["left", nt, b // 2][:, b % 2, :], in0=live["cube", step - 1][:],
+                    scalar=rise[:, b : b + 1], in1=live["above", step][:],
+                    op0=ALU.mult, op1=ALU.subtract,
                 )
-
-        def right_stage(step):
-            width = piece_x(step)[1]
-            j = step % KNOTS
-            if j == 4:
-                live["right"] = sides.tile([P, NB, D], BF16, name="right")
             if j >= 4:
                 b = j - 4
+                if b % 2 == 0:
+                    right = planes.tile([P, 2, width], BF16)
+                    live["right", nt, b // 2] = right
                 nc.vector.scalar_tensor_tensor(
-                    out=live["right"][:, b, :width], in0=live["fall", step - 1][:, :width],
-                    scalar=consts["neg_right_ratio"][:, b : b + 1],
-                    in1=live["fall", step][:, :width], op0=ALU.mult, op1=ALU.add,
+                    out=live["right", nt, b // 2][:, b % 2, :], in0=live["cube", step][:],
+                    scalar=neg_fall[:, b + 1 : b + 2], in1=live["below", step - 1][:],
+                    op0=ALU.mult, op1=ALU.subtract,
                 )
 
-        def silu_stage(nt):
-            silu = acts_pool.tile([P, 2, D // 2], BF16)
-            nc.scalar.activation(
-                out=silu[:], in_=x_sb[:, nt, :].rearrange("p (q e) -> p e q", e=2), func=ACT.Silu
+        def join_stage(nt, m):
+            bases = stage.tile([P, width, 2], BF16, align_bytes=64, name="bases")
+            nc.vector.scalar_tensor_tensor(
+                out=bases[:], in0=live["left", nt, m][:].rearrange("p e q -> p q e"), scalar=0.0,
+                in1=live["right", nt, m][:].rearrange("p e q -> p q e"), op0=ALU.max, op1=ALU.max,
             )
-            live["silu", nt] = silu
+            live["bases", nt, m] = bases
 
-        def join_stage(piece):
-            nt, first_feature, width = pieces[piece]
-            for first in range(0, width, P):
-                block = live["bases", nt][:, :, first_feature + first : first_feature + first + P]
-                nc.vector.tensor_tensor(
-                    out=block, in0=block, in1=live["right"][:, :, first : first + P], op=ALU.max
-                )
+        def bases_quantise_stage(nt, m):
+            passes = slice(1 + 2 * m, 3 + 2 * m)
+            nc.vector.quantize_mx(
+                out=a_codes[:, nt, passes, :].rearrange("p g n -> p (g n)").bitcast(FP8X4),
+                scales=a_scales[:, nt, passes, :].rearrange("p g n -> p (g n)"),
+                in_=live["bases", nt, m][:].rearrange("p q e -> p (q e)"),
+            )
 
-        def weight_bank_stage(ft, first_pass, n_pass, g, half):
-            rows = slice(ft * ROWS_PER_F_TILE, (ft + 1) * ROWS_PER_F_TILE)
-            if g == first_pass and half == 0:
-                raw = loads.tile([P, ROWS_PER_F_TILE, LOAD_PASSES * K_PASS], BF16, tag="w_raw")
-                if first_pass == 0:
-                    nc.sync.dma_start(out=raw[:, :, :K_PASS], in_=base_rows[:, rows, :])
+        def weight_bank_stage(kind, ft, half, h, m):
+            first_row = ft * ROWS_PER_F_TILE + half * ROWS_PER_BANK
+            rows = slice(first_row, first_row + ROWS_PER_BANK)
+            if m == 0:
+                raw = loads.tile([P, ROWS_PER_BANK, HALF * NB], BF16, tag="w_raw")
+                if kind == "base":
+                    nc.sync.dma_start(out=raw[:, :, :D], in_=base_rows[:, rows, :])
                 else:
-                    first = (first_pass - 1) * K_PASS
-                    nc.sync.dma_start(
-                        out=raw[:], in_=spline_rows[:, rows, first : first + n_pass * K_PASS]
-                    )
-                live["w_words"] = raw[:].bitcast(F32)
+                    cols = slice(h * HALF * NB, (h + 1) * HALF * NB)
+                    nc.sync.dma_start(out=raw[:], in_=spline_rows[:, rows, cols])
+                live["w_words", half] = raw[:].bitcast(F32)
+            g = 0 if kind == "base" else 1 + 2 * m + h
             if half == 0:
                 live["w_grouped", ft, g] = stage.tile(
                     [P, F_TILE, PACK], BF16, align_bytes=64, name="w_grouped", bufs=3
                 )
-            flipped = flips.tile([P, 2, 2 * P], F32, tag="flip")
-            for a in range(2):
+            flipped = flips.tile([P, 2, ROWS_PER_BANK * P], F32, tag="flip")
+            for a in range(ROWS_PER_BANK):
                 for u in range(2):
-                    if first_pass == 0:
+                    if kind == "base":
                         words = slice(u * P, (u + 1) * P)
                     else:
-                        words = slice(2 * (g - first_pass) + u, PACK * P, PACK)
+                        words = slice(PAIRS * P * u + m, PAIRS * P * (u + 1), PAIRS)
                     nc.tensor.transpose(
-                        flipped[:, u, a * P : (a + 1) * P],
-                        live["w_words"][:, 2 * half + a, words],
+                        flipped[:, u, a * P : (a + 1) * P], live["w_words", half][:, a, words],
                         ident_f32[:],
                     )
+            first_col = half * ROWS_PER_BANK * P
             nc.scalar.copy(
-                out=live["w_grouped", ft, g][:, half * 2 * P : (half + 1) * 2 * P, :].bitcast(F32),
+                out=live["w_grouped", ft, g][
+                    :, first_col : first_col + ROWS_PER_BANK * P, :
+                ].bitcast(F32),
                 in_=flipped[:].rearrange("p u f -> p f u"),
             )
 
@@ -298,39 +290,19 @@ def tile_kanblock_pa_kernel(tc, x, grid, w1_base, w1_spline, out):
                 in_=live["w_grouped", ft, g][:].rearrange("p f t -> p (f t)"),
             )
 
-        def flip_stage(nt, g0, n_pass):
-            flipped = flips.tile([P, LOAD_PASSES, PACK, P], BF16, tag="flip")
-            for g in range(n_pass):
-                for t in range(PACK):
-                    if g0 == 0:
-                        source = live["silu", nt][:, t % 2, (t // 2) * P : (t // 2 + 1) * P]
-                    else:
-                        first = (g0 - 1) // LOAD_PASSES * P
-                        source = live["bases", nt][:, PACK * g + t, first : first + P]
-                    nc.tensor.transpose(flipped[:, g, t, :], source, ident_bf[:])
-            live["a_flipped", nt, g0] = flipped
-
-        def group_stage(nt, g0, n_pass):
-            grouped = stage.tile([P, LOAD_PASSES, P, PACK], BF16, align_bytes=64, name="a_grouped")
-            nc.scalar.copy(
-                out=grouped[:, :n_pass],
-                in_=live["a_flipped", nt, g0][:, :n_pass].rearrange("p g t n -> p g n t"),
-            )
-            live["a_grouped", nt, g0] = grouped
-
-        def multiply_stage(nt, g0, n_pass):
-            nc.vector.quantize_mx(
-                out=a_codes[:, nt, g0 : g0 + n_pass, :].rearrange("p g n -> p (g n)").bitcast(FP8X4),
-                scales=a_scales[:, nt, g0 : g0 + n_pass, :].rearrange("p g n -> p (g n)"),
-                in_=live["a_grouped", nt, g0][:, :n_pass].rearrange("p g n t -> p (g n t)"),
-            )
-            for ft in range(F_TILES):
-                if g0 == 0:
-                    live["acc", ft] = sums.tile([P, F_TILE], F32, name="acc%d" % ft)
+        def multiply_stage(nt, m0, m1, fts):
+            first = 0 if m0 < 0 else 1 + 2 * m0
+            last = 2 + 2 * m1
+            if m1 < 0:
+                last = 0
+            for ft in range(fts[0], fts[1]):
+                if first == 0:
+                    acc = sums.tile([P, F_TILE], F32)
+                    live["acc", nt, ft] = acc
                 cols = slice(ft * F_TILE, (ft + 1) * F_TILE)
-                for g in range(g0, g0 + n_pass):
+                for g in range(first, last + 1):
                     nc.tensor.matmul_mx(
-                        out=live["acc", ft][:],
+                        out=live["acc", nt, ft][:],
                         lhsT=a_codes[:, nt, g, :].bitcast(FP8X4),
                         lhsT_scale=a_scales[:, nt, g, :],
                         rhs=w_codes[:, g, cols].bitcast(FP8X4),
@@ -339,44 +311,52 @@ def tile_kanblock_pa_kernel(tc, x, grid, w1_base, w1_spline, out):
                         stop=(g == PASSES - 1),
                     )
 
-        def store_stage(nt):
-            for ft in range(F_TILES):
+        def store_stage(nt, fts):
+            for ft in range(fts[0], fts[1]):
                 cols = slice(ft * F_TILE, (ft + 1) * F_TILE)
                 result = results.tile([P, F_TILE], F32)
-                if ft % 2 == 0 or nt < TOKEN_TILES - 1:
-                    nc.scalar.copy(out=result[:], in_=live["acc", ft][:])
+                if ft % 2 == 0 or nt < last_tile:
+                    nc.scalar.copy(out=result[:], in_=live["acc", nt, ft][:])
                 else:
-                    nc.vector.tensor_copy(out=result[:], in_=live["acc", ft][:])
+                    nc.vector.tensor_copy(out=result[:], in_=live["acc", nt, ft][:])
                 nc.sync.dma_start(out=out[nt * P : (nt + 1) * P, cols], in_=result[:])
 
+        turn_stage(0)
         square_stage(0)
+        rise, rise_inner, neg_fall, neg_fall_inner = spline_factors(nc, const, knots)
         for step in range(last_step + 1):
+            nt, j = divmod(step, KNOTS)
             if step + 1 < n_steps:
+                if (step + 1) % KNOTS == 0:
+                    turn_stage(nt + 1)
                 square_stage(step + 1)
             if step < n_steps:
                 cube_stage(step)
-                if step % KNOTS == 0 and pieces[step // KNOTS][1] == 0:
-                    silu_stage(pieces[step // KNOTS][0])
-            for begin, nt, g0, n_pass in slices:
+                if j == 0:
+                    silu_stage(nt)
+                if j == 1:
+                    silu_quantise_stage(nt)
+            for kind, ft, half, h, m in banks[step * BANKS_PER_STEP : (step + 1) * BANKS_PER_STEP]:
+                weight_bank_stage(kind, ft, half, h, m)
+            if step > 0:
+                for kind, ft, half, h, m in banks[
+                    (step - 1) * BANKS_PER_STEP : step * BANKS_PER_STEP
+                ]:
+                    if half == 1:
+                        weight_quantise_stage(ft, 0 if kind == "base" else 1 + 2 * m + h)
+            for begin, of_tile, m0, m1, fts in products:
                 if begin == step:
-                    flip_stage(nt, g0, n_pass)
-                if begin == step - 1:
-                    group_stage(nt, g0, n_pass)
-            for bank_step, ft, first_pass, n_pass, g, half in banks:
-                if bank_step == step:
-                    weight_bank_stage(ft, first_pass, n_pass, g, half)
-                if bank_step == step - 1 and half == 1:
-                    weight_quantise_stage(ft, g)
-            for begin, nt, g0, n_pass in slices:
-                if begin == step - 2:
-                    multiply_stage(nt, g0, n_pass)
-                if begin == step - 4 and g0 + n_pass == PASSES:
-                    store_stage(nt)
+                    multiply_stage(of_tile, m0, m1, fts)
+                if begin == step - 1 and m1 == PAIRS - 1:
+                    store_stage(of_tile, fts)
             if 1 <= step <= n_steps:
-                left_stage(step - 1)
-                right_stage(step - 1)
-            if KNOTS <= step <= n_steps and step % KNOTS == 0:
-                join_stage(step // KNOTS - 1)
+                side_stage(step - 1)
+            for m in range(PAIRS):
+                done, j_join = divmod(step - 2 - (2 * m + 5), KNOTS)
+                if j_join == 0 and 0 <= done < TOKEN_TILES:
+                    join_stage(done, m)
+                done, j_quantise = divmod(step - 3 - (2 * m + 5), KNOTS)
+                if j_quantise == 0 and 0 <= done < TOKEN_TILES:
+                    bases_quantise_stage(done, m)
             if step < n_steps:
-                rise_stage(step)
-                fall_stage(step)
+                inner_stage(step)

@@ -29,7 +29,11 @@ ROWS_PER_F_TILE = F_TILE // P
 ROWS_PER_BANK = 2
 HALF = D // 2
 
-BANKS_PER_STEP = 2
+CHUNKS = (2, 1, 1)
+VECTOR_BELOW = 6
+FIRST_BANK_BEAT = 2
+BANKS_PER_RUN = 12
+BEATS_PER_RUN = 5
 FLOPS = 2 * TOKENS * F_OUT * K_ALL
 
 
@@ -38,43 +42,46 @@ def spline_knots(nc, const, grid):
     nc.scalar.dma_start(out=knots_bf[:], in_=grid.partition_broadcast(P))
     knots = const.tile([P, KNOTS], F32)
     nc.vector.tensor_copy(out=knots[:], in_=knots_bf[:])
-    neg_knots = const.tile([P, KNOTS], F32)
-    nc.vector.tensor_scalar_mul(out=neg_knots[:], in0=knots[:], scalar1=-1.0)
-    return knots, neg_knots
+    return knots
 
 
 def spline_factors(nc, const, knots):
-    gap1 = const.tile([P, KNOTS - 1], F32)
-    nc.vector.tensor_sub(out=gap1[:], in0=knots[:, 1:], in1=knots[:, : KNOTS - 1])
-    gap2 = const.tile([P, KNOTS - 2], F32)
-    nc.vector.tensor_sub(out=gap2[:], in0=knots[:, 2:], in1=knots[:, : KNOTS - 2])
-    gap3 = const.tile([P, KNOTS - 3], F32)
-    nc.vector.tensor_sub(out=gap3[:], in0=knots[:, 3:], in1=knots[:, : KNOTS - 3])
-    gap4 = const.tile([P, KNOTS - 4], F32)
-    nc.vector.tensor_sub(out=gap4[:], in0=knots[:, 4:], in1=knots[:, : KNOTS - 4])
-
     n_cubes = KNOTS - 3
-    rise_den = const.tile([P, n_cubes], F32)
-    nc.vector.tensor_mul(out=rise_den[:], in0=gap1[:, :n_cubes], in1=gap2[:, :n_cubes])
-    nc.vector.tensor_mul(out=rise_den[:], in0=rise_den[:], in1=gap3[:])
-    rise = const.tile([P, n_cubes], F32)
-    nc.vector.reciprocal(out=rise[:], in_=rise_den[:])
-    fall_den = const.tile([P, n_cubes], F32)
-    nc.vector.tensor_mul(out=fall_den[:], in0=gap1[:, 2:], in1=gap2[:, 1:])
-    nc.vector.scalar_tensor_tensor(
-        out=fall_den[:], in0=fall_den[:], scalar=-1.0, in1=gap3[:], op0=ALU.mult, op1=ALU.mult
-    )
-    neg_fall = const.tile([P, n_cubes], F32)
-    nc.vector.reciprocal(out=neg_fall[:], in_=fall_den[:])
+    fall_at = n_cubes
+    gap1_at = 2 * n_cubes
+    den = const.tile([P, gap1_at + KNOTS - 1], F32)
+    gap1 = den[:, gap1_at:]
+    nc.gpsimd.tensor_sub(out=gap1, in0=knots[:, 1:], in1=knots[:, : KNOTS - 1])
+    gap2 = const.tile([P, KNOTS - 2], F32)
+    nc.gpsimd.tensor_sub(out=gap2[:], in0=knots[:, 2:], in1=knots[:, : KNOTS - 2])
+    gap3 = const.tile([P, KNOTS - 3], F32)
+    nc.gpsimd.tensor_sub(out=gap3[:], in0=knots[:, 3:], in1=knots[:, : KNOTS - 3])
+    neg_gap3 = const.tile([P, KNOTS - 3], F32)
+    nc.gpsimd.tensor_sub(out=neg_gap3[:], in0=knots[:, : KNOTS - 3], in1=knots[:, 3:])
+    gap4 = const.tile([P, KNOTS - 4], F32)
+    nc.gpsimd.tensor_sub(out=gap4[:], in0=knots[:, 4:], in1=knots[:, : KNOTS - 4])
 
-    inv_gap1 = const.tile([P, KNOTS - 1], F32)
-    nc.vector.reciprocal(out=inv_gap1[:], in_=gap1[:])
+    rise_pair = const.tile([P, n_cubes], F32)
+    nc.gpsimd.tensor_mul(out=rise_pair[:], in0=den[:, gap1_at : gap1_at + n_cubes], in1=gap2[:, :n_cubes])
+    nc.gpsimd.tensor_mul(out=den[:, :fall_at], in0=rise_pair[:], in1=gap3[:])
+    fall_pair = const.tile([P, n_cubes], F32)
+    nc.gpsimd.tensor_mul(out=fall_pair[:], in0=den[:, gap1_at + 2 :], in1=gap2[:, 1:])
+    nc.gpsimd.tensor_mul(out=den[:, fall_at:gap1_at], in0=fall_pair[:], in1=neg_gap3[:])
+    inverse = const.tile([P, gap1_at + KNOTS - 1], F32)
+    nc.vector.reciprocal(out=inverse[:], in_=den[:])
+    rise = inverse[:, :fall_at]
+    neg_fall = inverse[:, fall_at:gap1_at]
+
+    rise_ratio = const.tile([P, NB], F32)
+    nc.gpsimd.tensor_mul(out=rise_ratio[:], in0=gap4[:], in1=inverse[:, gap1_at : gap1_at + NB])
     rise_inner = const.tile([P, NB], F32)
-    nc.vector.tensor_mul(out=rise_inner[:], in0=gap4[:], in1=inv_gap1[:, :NB])
-    nc.vector.tensor_mul(out=rise_inner[:], in0=rise_inner[:], in1=rise[:, 1:])
+    nc.gpsimd.tensor_mul(out=rise_inner[:], in0=rise_ratio[:], in1=inverse[:, 1:fall_at])
+    fall_ratio = const.tile([P, NB], F32)
+    nc.gpsimd.tensor_mul(out=fall_ratio[:], in0=gap4[:], in1=inverse[:, gap1_at + 3 :])
     neg_fall_inner = const.tile([P, NB], F32)
-    nc.vector.tensor_mul(out=neg_fall_inner[:], in0=gap4[:], in1=inv_gap1[:, 3:])
-    nc.vector.tensor_mul(out=neg_fall_inner[:], in0=neg_fall_inner[:], in1=neg_fall[:, :NB])
+    nc.gpsimd.tensor_mul(
+        out=neg_fall_inner[:], in0=fall_ratio[:], in1=inverse[:, fall_at : fall_at + NB]
+    )
     return rise, rise_inner, neg_fall, neg_fall_inner
 
 
@@ -84,8 +91,11 @@ def tile_kanblock_pa_kernel(tc, x, grid, w1_base, w1_spline, out):
     base_rows = w1_base.rearrange("(a p) k -> p a k", p=P)
     spline_rows = w1_spline.rearrange("(a p) i b -> p a (i b)", p=P)
 
-    width = PACK * P
-    n_steps = KNOTS * TOKEN_TILES
+    n_steps = KNOTS * len(CHUNKS)
+    first_tile = [sum(CHUNKS[:c]) for c in range(len(CHUNKS))]
+    last_tile = TOKEN_TILES - 1
+    last_chunk = len(CHUNKS) - 1
+    last_pair = (last_chunk, PAIRS - 1)
 
     banks = []
     for ft in range(F_TILES):
@@ -95,156 +105,209 @@ def tile_kanblock_pa_kernel(tc, x, grid, w1_base, w1_spline, out):
             for m in range(PAIRS):
                 for half in range(2):
                     banks.append(("spline", ft, half, h, m))
+    step_of_beat = []
+    for c, tiles in enumerate(CHUNKS):
+        for j in range(KNOTS):
+            step_of_beat += tiles * [KNOTS * c + j]
+
+    def bank_step(i):
+        return step_of_beat[FIRST_BANK_BEAT + i * BEATS_PER_RUN // BANKS_PER_RUN]
+
     weights_done = [
-        ((ft + 1) * len(banks) // F_TILES - 1) // BANKS_PER_STEP + 1 for ft in range(F_TILES)
+        bank_step((ft + 1) * len(banks) // F_TILES - 1) + 1 for ft in range(F_TILES)
     ]
 
-    last_tile = TOKEN_TILES - 1
     ready = []
-    for nt in range(last_tile):
-        for ft in range(F_TILES):
-            made = KNOTS * nt + 2 * PAIRS + 6
-            ready.append((max(made, weights_done[ft]) + 1, nt, -1, PAIRS - 1, (ft, ft + 1)))
-    for m in range(-1, PAIRS):
-        made = KNOTS * last_tile + (2 if m < 0 else 2 * m + 8)
-        ready.append((max(made, KNOTS * last_tile + 8) + 1, last_tile, m, m, (0, F_TILES)))
+    for c in range(last_chunk):
+        for nt in range(first_tile[c], first_tile[c] + CHUNKS[c]):
+            for ft in range(F_TILES):
+                made = KNOTS * c + 2 * PAIRS + 5
+                ready.append((max(made, weights_done[ft]) + 1, nt, ft))
     products = []
     free_step = 0
-    for begin, nt, m0, m1, fts in sorted(ready):
+    for begin, nt, ft in sorted(ready):
         begin = max(begin, free_step)
-        products.append((begin, nt, m0, m1, fts))
+        if begin <= weights_done[F_TILES - 1]:
+            products.append((begin, nt, 0, PASSES // 2 - 1, (ft, ft + 1)))
+            products.append((begin + 1, nt, PASSES // 2, PASSES - 1, (ft, ft + 1)))
+        else:
+            products.append((begin, nt, 0, PASSES - 1, (ft, ft + 1)))
+        free_step = products[-1][0] + 1
+    for m in range(-1, PAIRS):
+        made = KNOTS * last_chunk + (2 if m < 0 else 2 * m + 7)
+        begin = max(made + 1, free_step)
+        products.append((begin, last_tile, max(0, 1 + 2 * m), 2 + 2 * m, (0, F_TILES)))
         free_step = begin + 1
     last_step = products[-1][0] + 1
 
     with ExitStack() as pools:
         const = pools.enter_context(tc.tile_pool(name="const", bufs=1))
         keep = pools.enter_context(tc.tile_pool(name="keep", bufs=1))
-        loads = pools.enter_context(tc.tile_pool(name="loads", bufs=4))
-        stage = pools.enter_context(tc.tile_pool(name="stage", bufs=3))
-        planes = pools.enter_context(tc.tile_pool(name="planes", bufs=4))
+        loads = pools.enter_context(tc.tile_pool(name="loads", bufs=3))
+        stage = pools.enter_context(tc.tile_pool(name="stage", bufs=2))
+        planes = pools.enter_context(tc.tile_pool(name="planes", bufs=3))
         results = pools.enter_context(tc.tile_pool(name="results", bufs=4))
-        flips = pools.enter_context(tc.psum_pool(name="flips", bufs=4))
-        sums = pools.enter_context(tc.psum_pool(name="sums", bufs=4))
+        psum = pools.enter_context(tc.psum_pool(name="psum", bufs=8))
 
         x_sb = const.tile([P, TOKEN_TILES, D], BF16)
-        for nt in range(TOKEN_TILES):
+        for nt in range(CHUNKS[0]):
             nc.sync.dma_start(out=x_sb[:, nt, :], in_=x_rows[:, nt, :])
-        knots, neg_knots = spline_knots(nc, const, grid)
+        knots = spline_knots(nc, const, grid)
         ident_f32 = const.tile([P, P], F32)
         make_identity(nc, ident_f32[:])
         ident_bf = const.tile([P, P], BF16)
         make_identity(nc, ident_bf[:])
 
-        x_t = const.tile([P, TOKEN_TILES, 2, P, 2], BF16)
-        a_codes = keep.tile([P, TOKEN_TILES, PASSES, P], U32, align_bytes=64)
-        a_scales = keep.tile([P, TOKEN_TILES, PASSES, P], U8, align_bytes=64)
+        x_t = const.tile([P, TOKENS * PACK], BF16)
+        a_codes = keep.tile([P, TOKENS * PASSES], U32, align_bytes=64)
+        a_scales = keep.tile([P, TOKENS * PASSES], U8, align_bytes=64)
         w_codes = keep.tile([P, PASSES, F_OUT], U32, align_bytes=64)
-        w_scales = keep.tile([P, PASSES, F_OUT], U8, align_bytes=64)
+        w_scales = keep.tile([P, (PASSES + 3) // 4, F_OUT], U8, align_bytes=64)
 
         live = {}
 
-        def turn_stage(nt):
-            turned = flips.tile([P, PACK, P], BF16, tag="flip")
-            for c in range(PACK):
-                nc.tensor.transpose(turned[:, c, :], x_sb[:, nt, c * P : (c + 1) * P], ident_bf[:])
-            nc.vector.tensor_scalar(
-                out=x_t[:, nt], in0=turned[:].rearrange("p (h u) n -> p h n u", u=2),
-                scalar1=knots[:, 0:1], scalar2=knots[:, KNOTS - 1 : KNOTS],
-                op0=ALU.max, op1=ALU.min,
-            )
+        def chunk_tokens(c):
+            return slice(first_tile[c] * P, (first_tile[c] + CHUNKS[c]) * P)
 
-        def silu_stage(nt):
-            words = x_sb[:, nt, :].bitcast(F32)
-            turned = flips.tile([P, 2, P], F32, tag="flip")
-            for u in range(2):
-                nc.tensor.transpose(turned[:, u, :], words[:, u * P : (u + 1) * P], ident_f32[:])
-            silu = stage.tile([P, P, PACK], BF16, align_bytes=64, name="silu", bufs=2)
-            nc.scalar.activation(
-                out=silu[:].rearrange("p n (u e) -> p n u e", u=2),
-                in_=turned[:].bitcast(BF16).rearrange("p u (n e) -> p n u e", e=2),
-                func=ACT.Silu,
-            )
-            live["silu", nt] = silu
+        def width_of(c):
+            return PACK * P * CHUNKS[c]
 
-        def silu_quantise_stage(nt):
+        def chunk_x(c):
+            tokens = chunk_tokens(c)
+            return x_t[:, PACK * tokens.start : PACK * tokens.stop]
+
+        def of_passes(tile, c):
+            tokens = chunk_tokens(c)
+            part = tile[:, PASSES * tokens.start : PASSES * tokens.stop]
+            return part.rearrange("p (g n) -> p g n", g=PASSES)
+
+        def w_scale_rows(g, cols):
+            return w_scales[4 * (g % 4) :, g // 4, cols]
+
+        def turn_stage(c):
+            for i in range(CHUNKS[c]):
+                nt = first_tile[c] + i
+                turned = psum.tile([P, PACK, P], BF16, tag="bank")
+                for f in range(PACK):
+                    nc.tensor.transpose(
+                        turned[:, f, :], x_sb[:, nt, f * P : (f + 1) * P], ident_bf[:]
+                    )
+                nc.vector.tensor_scalar(
+                    out=chunk_x(c).rearrange("p (h n u) -> p h n u", h=2, u=2)[
+                        :, :, i * P : (i + 1) * P, :
+                    ],
+                    in0=turned[:].rearrange("p (h u) n -> p h n u", u=2),
+                    scalar1=knots[:, 0:1], scalar2=knots[:, KNOTS - 1 : KNOTS],
+                    op0=ALU.max, op1=ALU.min,
+                )
+
+        def silu_stage(c):
+            silu = stage.tile([P, CHUNKS[c] * P, PACK], BF16, align_bytes=64, name="silu")
+            for i in range(CHUNKS[c]):
+                words = x_sb[:, first_tile[c] + i, :].bitcast(F32)
+                turned = psum.tile([P, 2, P], F32, tag="bank")
+                for u in range(2):
+                    nc.tensor.transpose(
+                        turned[:, u, :], words[:, u * P : (u + 1) * P], ident_f32[:]
+                    )
+                nc.scalar.activation(
+                    out=silu[:, i * P : (i + 1) * P, :].rearrange("p n (u e) -> p n u e", u=2),
+                    in_=turned[:].bitcast(BF16).rearrange("p u (n e) -> p n u e", e=2),
+                    func=ACT.Silu,
+                )
+            live["silu", c] = silu
+
+        def silu_quantise_stage(c):
             nc.vector.quantize_mx(
-                out=a_codes[:, nt, 0, :].bitcast(FP8X4),
-                scales=a_scales[:, nt, 0, :],
-                in_=live["silu", nt][:].rearrange("p n t -> p (n t)"),
+                out=of_passes(a_codes, c)[:, 0, :].bitcast(FP8X4),
+                scales=of_passes(a_scales, c)[:, 0, :],
+                in_=live["silu", c][:].rearrange("p n t -> p (n t)"),
             )
-
-        def tile_x(step):
-            return x_t[:, step // KNOTS].rearrange("p h n u -> p (h n u)")
 
         def square_stage(step):
-            j = step % KNOTS
-            square = planes.tile([P, width], F32)
+            c, j = divmod(step, KNOTS)
+            square = planes.tile([P, width_of(c)], F32, bufs=2)
             nc.scalar.activation(
-                out=square[:], in_=tile_x(step), func=ACT.Square,
-                bias=neg_knots[:, j : j + 1], scale=1.0,
+                out=square[:], in_=chunk_x(c), func=ACT.Square,
+                bias=knots[:, j : j + 1], scale=-1.0,
             )
             live["square", step] = square
 
         def cube_stage(step):
-            j = step % KNOTS
-            cube = planes.tile([P, width], F32)
+            c, j = divmod(step, KNOTS)
+            cube = planes.tile([P, width_of(c)], F32)
             nc.vector.scalar_tensor_tensor(
-                out=cube[:], in0=tile_x(step), scalar=knots[:, j : j + 1],
+                out=cube[:], in0=chunk_x(c), scalar=knots[:, j : j + 1],
                 in1=live["square", step][:], op0=ALU.subtract, op1=ALU.mult,
             )
             live["cube", step] = cube
 
         def inner_stage(step):
-            j = step % KNOTS
+            c, j = divmod(step, KNOTS)
             cube = live["cube", step]
             if 1 <= j <= NB:
-                above = planes.tile([P, width], F32)
-                factor = rise_inner[:, j - 1 : j]
-                nc.scalar.activation(out=above[:], in_=cube[:], func=ACT.Relu, scale=factor)
+                above = planes.tile([P, width_of(c)], F32, bufs=2)
+                nc.scalar.activation(
+                    out=above[:], in_=cube[:], func=ACT.Relu, scale=rise_inner[:, j - 1 : j]
+                )
                 live["above", step] = above
             if 3 <= j <= NB + 2:
-                below = planes.tile([P, width], F32)
+                below = planes.tile([P, width_of(c)], F32)
                 factor = neg_fall_inner[:, j - 3 : j - 2]
-                nc.scalar.activation(out=below[:], in_=cube[:], func=ACT.Relu, scale=factor)
+                if c == 0 and j < VECTOR_BELOW:
+                    nc.vector.tensor_scalar(
+                        out=below[:], in0=cube[:], scalar1=0.0, scalar2=factor,
+                        op0=ALU.min, op1=ALU.mult,
+                    )
+                else:
+                    nc.scalar.activation(out=below[:], in_=cube[:], func=ACT.Relu, scale=factor)
                 live["below", step] = below
 
         def side_stage(step):
-            nt, j = divmod(step, KNOTS)
+            c, j = divmod(step, KNOTS)
             if 1 <= j <= NB:
                 b = j - 1
                 if b % 2 == 0:
-                    left = planes.tile([P, 2, width], BF16)
-                    live["left", nt, b // 2] = left
+                    left = planes.tile([P, 2, width_of(c)], BF16)
+                    live["left", c, b // 2] = left
                 nc.vector.scalar_tensor_tensor(
-                    out=live["left", nt, b // 2][:, b % 2, :], in0=live["cube", step - 1][:],
+                    out=live["left", c, b // 2][:, b % 2, :], in0=live["cube", step - 1][:],
                     scalar=rise[:, b : b + 1], in1=live["above", step][:],
                     op0=ALU.mult, op1=ALU.subtract,
                 )
             if j >= 4:
                 b = j - 4
                 if b % 2 == 0:
-                    right = planes.tile([P, 2, width], BF16)
-                    live["right", nt, b // 2] = right
+                    right = planes.tile([P, 2, width_of(c)], BF16, bufs=2)
+                    live["right", c, b // 2] = right
                 nc.vector.scalar_tensor_tensor(
-                    out=live["right", nt, b // 2][:, b % 2, :], in0=live["cube", step][:],
+                    out=live["right", c, b // 2][:, b % 2, :], in0=live["cube", step][:],
                     scalar=neg_fall[:, b + 1 : b + 2], in1=live["below", step - 1][:],
                     op0=ALU.mult, op1=ALU.subtract,
                 )
 
-        def join_stage(nt, m):
-            bases = stage.tile([P, width, 2], BF16, align_bytes=64, name="bases")
-            nc.vector.scalar_tensor_tensor(
-                out=bases[:], in0=live["left", nt, m][:].rearrange("p e q -> p q e"), scalar=0.0,
-                in1=live["right", nt, m][:].rearrange("p e q -> p q e"), op0=ALU.max, op1=ALU.max,
-            )
-            live["bases", nt, m] = bases
+        def join_stage(c, m):
+            bases = stage.tile([P, width_of(c), 2], BF16, align_bytes=64, name="bases")
+            live["bases", c, m] = bases
+            parts = [slice(0, 1), slice(1, 2)] if (c, m) == last_pair else [slice(0, 2)]
+            for h in parts:
+                qs = slice(h.start * width_of(c) // 2, h.stop * width_of(c) // 2)
+                nc.vector.scalar_tensor_tensor(
+                    out=bases[:, qs, :],
+                    in0=live["left", c, m][:, :, qs].rearrange("p e q -> p q e"), scalar=0.0,
+                    in1=live["right", c, m][:, :, qs].rearrange("p e q -> p q e"),
+                    op0=ALU.max, op1=ALU.max,
+                )
+                if (c, m) == last_pair:
+                    bases_quantise_stage(c, m, h)
 
-        def bases_quantise_stage(nt, m):
-            passes = slice(1 + 2 * m, 3 + 2 * m)
+        def bases_quantise_stage(c, m, h):
+            qs = slice(h.start * width_of(c) // 2, h.stop * width_of(c) // 2)
+            passes = slice(1 + 2 * m + h.start, 1 + 2 * m + h.stop)
             nc.vector.quantize_mx(
-                out=a_codes[:, nt, passes, :].rearrange("p g n -> p (g n)").bitcast(FP8X4),
-                scales=a_scales[:, nt, passes, :].rearrange("p g n -> p (g n)"),
-                in_=live["bases", nt, m][:].rearrange("p q e -> p (q e)"),
+                out=of_passes(a_codes, c)[:, passes, :].rearrange("p g n -> p (g n)").bitcast(FP8X4),
+                scales=of_passes(a_scales, c)[:, passes, :].rearrange("p g n -> p (g n)"),
+                in_=live["bases", c, m][:, qs, :].rearrange("p q e -> p (q e)"),
             )
 
         def weight_bank_stage(kind, ft, half, h, m):
@@ -263,7 +326,7 @@ def tile_kanblock_pa_kernel(tc, x, grid, w1_base, w1_spline, out):
                 live["w_grouped", ft, g] = stage.tile(
                     [P, F_TILE, PACK], BF16, align_bytes=64, name="w_grouped", bufs=3
                 )
-            flipped = flips.tile([P, 2, ROWS_PER_BANK * P], F32, tag="flip")
+            flipped = psum.tile([P, 2, ROWS_PER_BANK * P], F32, tag="bank")
             for a in range(ROWS_PER_BANK):
                 for u in range(2):
                     if kind == "base":
@@ -286,30 +349,30 @@ def tile_kanblock_pa_kernel(tc, x, grid, w1_base, w1_spline, out):
             cols = slice(ft * F_TILE, (ft + 1) * F_TILE)
             nc.vector.quantize_mx(
                 out=w_codes[:, g, cols].bitcast(FP8X4),
-                scales=w_scales[:, g, cols],
+                scales=w_scale_rows(g, cols),
                 in_=live["w_grouped", ft, g][:].rearrange("p f t -> p (f t)"),
             )
 
-        def multiply_stage(nt, m0, m1, fts):
-            first = 0 if m0 < 0 else 1 + 2 * m0
-            last = 2 + 2 * m1
-            if m1 < 0:
-                last = 0
-            for ft in range(fts[0], fts[1]):
-                if first == 0:
-                    acc = sums.tile([P, F_TILE], F32)
+        def multiply_stage(nt, first, last, fts):
+            order = [(ft, g) for ft in range(fts[0], fts[1]) for g in range(first, last + 1)]
+            if nt == last_tile:
+                order = [(ft, g) for g in range(first, last + 1) for ft in range(fts[0], fts[1])]
+            c = max(c for c in range(len(CHUNKS)) if first_tile[c] <= nt)
+            tokens = slice((nt - first_tile[c]) * P, (nt - first_tile[c] + 1) * P)
+            for ft, g in order:
+                if g == 0:
+                    acc = psum.tile([P, F_TILE], F32, tag="bank")
                     live["acc", nt, ft] = acc
                 cols = slice(ft * F_TILE, (ft + 1) * F_TILE)
-                for g in range(first, last + 1):
-                    nc.tensor.matmul_mx(
-                        out=live["acc", nt, ft][:],
-                        lhsT=a_codes[:, nt, g, :].bitcast(FP8X4),
-                        lhsT_scale=a_scales[:, nt, g, :],
-                        rhs=w_codes[:, g, cols].bitcast(FP8X4),
-                        rhs_scale=w_scales[:, g, cols],
-                        start=(g == 0),
-                        stop=(g == PASSES - 1),
-                    )
+                nc.tensor.matmul_mx(
+                    out=live["acc", nt, ft][:],
+                    lhsT=of_passes(a_codes, c)[:, g, tokens].bitcast(FP8X4),
+                    lhsT_scale=of_passes(a_scales, c)[:, g, tokens],
+                    rhs=w_codes[:, g, cols].bitcast(FP8X4),
+                    rhs_scale=w_scale_rows(g, cols),
+                    start=(g == 0),
+                    stop=(g == PASSES - 1),
+                )
 
         def store_stage(nt, fts):
             for ft in range(fts[0], fts[1]):
@@ -321,42 +384,48 @@ def tile_kanblock_pa_kernel(tc, x, grid, w1_base, w1_spline, out):
                     nc.vector.tensor_copy(out=result[:], in_=live["acc", nt, ft][:])
                 nc.sync.dma_start(out=out[nt * P : (nt + 1) * P, cols], in_=result[:])
 
-        turn_stage(0)
+        def banks_of(step):
+            return [bank for i, bank in enumerate(banks) if bank_step(i) == step]
+
+        with tc.manual_schedule(engines={mybir.EngineType.DVE}):
+            turn_stage(0)
+            rise, rise_inner, neg_fall, neg_fall_inner = spline_factors(nc, const, knots)
         square_stage(0)
-        rise, rise_inner, neg_fall, neg_fall_inner = spline_factors(nc, const, knots)
         for step in range(last_step + 1):
-            nt, j = divmod(step, KNOTS)
+            c, j = divmod(step, KNOTS)
             if step + 1 < n_steps:
                 if (step + 1) % KNOTS == 0:
-                    turn_stage(nt + 1)
+                    turn_stage(c + 1)
                 square_stage(step + 1)
             if step < n_steps:
                 cube_stage(step)
+            for m in range(PAIRS):
+                done, j_join = divmod(step - 2 - (2 * m + 5), KNOTS)
+                if j_join == 0 and 0 <= done < len(CHUNKS):
+                    join_stage(done, m)
+            if step < n_steps:
                 if j == 0:
-                    silu_stage(nt)
+                    silu_stage(c)
                 if j == 1:
-                    silu_quantise_stage(nt)
-            for kind, ft, half, h, m in banks[step * BANKS_PER_STEP : (step + 1) * BANKS_PER_STEP]:
+                    silu_quantise_stage(c)
+            for kind, ft, half, h, m in banks_of(step):
                 weight_bank_stage(kind, ft, half, h, m)
-            if step > 0:
-                for kind, ft, half, h, m in banks[
-                    (step - 1) * BANKS_PER_STEP : step * BANKS_PER_STEP
-                ]:
-                    if half == 1:
-                        weight_quantise_stage(ft, 0 if kind == "base" else 1 + 2 * m + h)
-            for begin, of_tile, m0, m1, fts in products:
+            if step == 0:
+                for later in range(CHUNKS[0], TOKEN_TILES):
+                    nc.sync.dma_start(out=x_sb[:, later, :], in_=x_rows[:, later, :])
+            for kind, ft, half, h, m in banks_of(step - 1):
+                if half == 1:
+                    weight_quantise_stage(ft, 0 if kind == "base" else 1 + 2 * m + h)
+            for begin, of_tile, first, last, fts in products:
                 if begin == step:
-                    multiply_stage(of_tile, m0, m1, fts)
-                if begin == step - 1 and m1 == PAIRS - 1:
+                    multiply_stage(of_tile, first, last, fts)
+                if begin == step - 1 and last == PASSES - 1:
                     store_stage(of_tile, fts)
             if 1 <= step <= n_steps:
                 side_stage(step - 1)
             for m in range(PAIRS):
                 done, j_join = divmod(step - 2 - (2 * m + 5), KNOTS)
-                if j_join == 0 and 0 <= done < TOKEN_TILES:
-                    join_stage(done, m)
-                done, j_quantise = divmod(step - 3 - (2 * m + 5), KNOTS)
-                if j_quantise == 0 and 0 <= done < TOKEN_TILES:
-                    bases_quantise_stage(done, m)
+                if j_join == 0 and 0 <= done < len(CHUNKS) and (done, m) != last_pair:
+                    bases_quantise_stage(done, m, slice(0, 2))
             if step < n_steps:
                 inner_stage(step)

@@ -30,7 +30,7 @@ ROWS_PER_BANK = 2
 HALF = D // 2
 
 CHUNKS = (2, 1, 1)
-VECTOR_BELOW = 6
+VECTOR_BELOW = 5
 FIRST_BANK_BEAT = 2
 BANKS_PER_RUN = 12
 BEATS_PER_RUN = 5
@@ -143,10 +143,9 @@ def tile_kanblock_pa_kernel(tc, x, grid, w1_base, w1_spline, out):
     with ExitStack() as pools:
         const = pools.enter_context(tc.tile_pool(name="const", bufs=1))
         keep = pools.enter_context(tc.tile_pool(name="keep", bufs=1))
-        loads = pools.enter_context(tc.tile_pool(name="loads", bufs=3))
+        loads = pools.enter_context(tc.tile_pool(name="loads", bufs=4))
         stage = pools.enter_context(tc.tile_pool(name="stage", bufs=2))
         planes = pools.enter_context(tc.tile_pool(name="planes", bufs=3))
-        results = pools.enter_context(tc.tile_pool(name="results", bufs=4))
         psum = pools.enter_context(tc.psum_pool(name="psum", bufs=8))
 
         x_sb = const.tile([P, TOKEN_TILES, D], BF16)
@@ -176,6 +175,9 @@ def tile_kanblock_pa_kernel(tc, x, grid, w1_base, w1_spline, out):
             tokens = chunk_tokens(c)
             return x_t[:, PACK * tokens.start : PACK * tokens.stop]
 
+        def by_token(plane):
+            return plane.rearrange("p (h n u) -> p h n u", h=2, u=2)
+
         def of_passes(tile, c):
             tokens = chunk_tokens(c)
             part = tile[:, PASSES * tokens.start : PASSES * tokens.stop]
@@ -193,16 +195,14 @@ def tile_kanblock_pa_kernel(tc, x, grid, w1_base, w1_spline, out):
                         turned[:, f, :], x_sb[:, nt, f * P : (f + 1) * P], ident_bf[:]
                     )
                 nc.vector.tensor_scalar(
-                    out=chunk_x(c).rearrange("p (h n u) -> p h n u", h=2, u=2)[
-                        :, :, i * P : (i + 1) * P, :
-                    ],
+                    out=by_token(chunk_x(c))[:, :, i * P : (i + 1) * P, :],
                     in0=turned[:].rearrange("p (h u) n -> p h n u", u=2),
                     scalar1=knots[:, 0:1], scalar2=knots[:, KNOTS - 1 : KNOTS],
                     op0=ALU.max, op1=ALU.min,
                 )
 
         def silu_stage(c):
-            silu = stage.tile([P, CHUNKS[c] * P, PACK], BF16, align_bytes=64, name="silu")
+            silu = stage.tile([P, CHUNKS[c] * P, PACK], BF16, align_bytes=64, name="silu", bufs=1)
             for i in range(CHUNKS[c]):
                 words = x_sb[:, first_tile[c] + i, :].bitcast(F32)
                 turned = psum.tile([P, 2, P], F32, tag="bank")
@@ -224,22 +224,35 @@ def tile_kanblock_pa_kernel(tc, x, grid, w1_base, w1_spline, out):
                 in_=live["silu", c][:].rearrange("p n t -> p (n t)"),
             )
 
+        def token_parts(step):
+            if step > 0:
+                return [lambda plane: plane]
+            columns = 2 * P
+            return [
+                lambda plane, i=i: plane.rearrange("p (h r) -> p h r", h=2)[
+                    :, :, i * columns : (i + 1) * columns
+                ]
+                for i in range(CHUNKS[0])
+            ]
+
         def square_stage(step):
             c, j = divmod(step, KNOTS)
             square = planes.tile([P, width_of(c)], F32, bufs=2)
-            nc.scalar.activation(
-                out=square[:], in_=chunk_x(c), func=ACT.Square,
-                bias=knots[:, j : j + 1], scale=-1.0,
-            )
+            for part in token_parts(step):
+                nc.scalar.activation(
+                    out=part(square[:]), in_=part(chunk_x(c)), func=ACT.Square,
+                    bias=knots[:, j : j + 1], scale=-1.0,
+                )
             live["square", step] = square
 
         def cube_stage(step):
             c, j = divmod(step, KNOTS)
             cube = planes.tile([P, width_of(c)], F32)
-            nc.vector.scalar_tensor_tensor(
-                out=cube[:], in0=chunk_x(c), scalar=knots[:, j : j + 1],
-                in1=live["square", step][:], op0=ALU.subtract, op1=ALU.mult,
-            )
+            for part in token_parts(step):
+                nc.vector.scalar_tensor_tensor(
+                    out=part(cube[:]), in0=part(chunk_x(c)), scalar=knots[:, j : j + 1],
+                    in1=part(live["square", step][:]), op0=ALU.subtract, op1=ALU.mult,
+                )
             live["cube", step] = cube
 
         def inner_stage(step):
@@ -289,9 +302,11 @@ def tile_kanblock_pa_kernel(tc, x, grid, w1_base, w1_spline, out):
         def join_stage(c, m):
             bases = stage.tile([P, width_of(c), 2], BF16, align_bytes=64, name="bases")
             live["bases", c, m] = bases
-            parts = [slice(0, 1), slice(1, 2)] if (c, m) == last_pair else [slice(0, 2)]
-            for h in parts:
-                qs = slice(h.start * width_of(c) // 2, h.stop * width_of(c) // 2)
+            parts = 1
+            if (c, m) == last_pair:
+                parts = 2
+            for part in range(parts):
+                qs = slice(part * width_of(c) // parts, (part + 1) * width_of(c) // parts)
                 nc.vector.scalar_tensor_tensor(
                     out=bases[:, qs, :],
                     in0=live["left", c, m][:, :, qs].rearrange("p e q -> p q e"), scalar=0.0,
@@ -299,7 +314,7 @@ def tile_kanblock_pa_kernel(tc, x, grid, w1_base, w1_spline, out):
                     op0=ALU.max, op1=ALU.max,
                 )
                 if (c, m) == last_pair:
-                    bases_quantise_stage(c, m, h)
+                    bases_quantise_stage(c, m, slice(part, part + 1))
 
         def bases_quantise_stage(c, m, h):
             qs = slice(h.start * width_of(c) // 2, h.stop * width_of(c) // 2)
@@ -324,7 +339,7 @@ def tile_kanblock_pa_kernel(tc, x, grid, w1_base, w1_spline, out):
             g = 0 if kind == "base" else 1 + 2 * m + h
             if half == 0:
                 live["w_grouped", ft, g] = stage.tile(
-                    [P, F_TILE, PACK], BF16, align_bytes=64, name="w_grouped", bufs=3
+                    [P, F_TILE, PACK], BF16, align_bytes=64, name="w_grouped", tag="wide", bufs=4
                 )
             flipped = psum.tile([P, 2, ROWS_PER_BANK * P], F32, tag="bank")
             for a in range(ROWS_PER_BANK):
@@ -377,7 +392,9 @@ def tile_kanblock_pa_kernel(tc, x, grid, w1_base, w1_spline, out):
         def store_stage(nt, fts):
             for ft in range(fts[0], fts[1]):
                 cols = slice(ft * F_TILE, (ft + 1) * F_TILE)
-                result = results.tile([P, F_TILE], F32)
+                result = stage.tile(
+                    [P, F_TILE], F32, align_bytes=64, name="result", tag="wide", bufs=4
+                )
                 if ft % 2 == 0 or nt < last_tile:
                     nc.scalar.copy(out=result[:], in_=live["acc", nt, ft][:])
                 else:
@@ -391,18 +408,27 @@ def tile_kanblock_pa_kernel(tc, x, grid, w1_base, w1_spline, out):
             turn_stage(0)
             rise, rise_inner, neg_fall, neg_fall_inner = spline_factors(nc, const, knots)
         square_stage(0)
+        tail_step = KNOTS * last_chunk + KNOTS - 3
         for step in range(last_step + 1):
             c, j = divmod(step, KNOTS)
+            if step == tail_step:
+                pools.enter_context(tc.manual_schedule(engines={mybir.EngineType.DVE}))
             if step + 1 < n_steps:
                 if (step + 1) % KNOTS == 0:
                     turn_stage(c + 1)
                 square_stage(step + 1)
+            if step > tail_step and step <= n_steps:
+                side_stage(step - 1)
             if step < n_steps:
                 cube_stage(step)
-            for m in range(PAIRS):
-                done, j_join = divmod(step - 2 - (2 * m + 5), KNOTS)
-                if j_join == 0 and 0 <= done < len(CHUNKS):
-                    join_stage(done, m)
+            made = [divmod(step - (1 if step > tail_step else 2) - (2 * m + 5), KNOTS)
+                    for m in range(PAIRS)]
+            joins = [(made_c, m) for m, (made_c, rest) in enumerate(made)
+                     if rest == 0 and 0 <= made_c < len(CHUNKS)]
+            for made_c, m in joins:
+                join_stage(made_c, m)
+                if made_c == last_chunk and (made_c, m) != last_pair:
+                    bases_quantise_stage(made_c, m, slice(0, 2))
             if step < n_steps:
                 if j == 0:
                     silu_stage(c)
@@ -421,11 +447,10 @@ def tile_kanblock_pa_kernel(tc, x, grid, w1_base, w1_spline, out):
                     multiply_stage(of_tile, first, last, fts)
                 if begin == step - 1 and last == PASSES - 1:
                     store_stage(of_tile, fts)
-            if 1 <= step <= n_steps:
+            if 1 <= step <= tail_step:
                 side_stage(step - 1)
-            for m in range(PAIRS):
-                done, j_join = divmod(step - 2 - (2 * m + 5), KNOTS)
-                if j_join == 0 and 0 <= done < len(CHUNKS) and (done, m) != last_pair:
-                    bases_quantise_stage(done, m, slice(0, 2))
+            for made_c, m in joins:
+                if made_c != last_chunk:
+                    bases_quantise_stage(made_c, m, slice(0, 2))
             if step < n_steps:
                 inner_stage(step)

@@ -30,7 +30,7 @@ ROWS_PER_BANK = 2
 HALF = D // 2
 
 CHUNKS = (2, 1, 1)
-VECTOR_BELOW = 5
+VECTOR_BELOW = 4
 FIRST_BANK_BEAT = 2
 BANKS_PER_RUN = 12
 BEATS_PER_RUN = 5
@@ -134,7 +134,7 @@ def tile_kanblock_pa_kernel(tc, x, grid, w1_base, w1_spline, out):
             products.append((begin, nt, 0, PASSES - 1, (ft, ft + 1)))
         free_step = products[-1][0] + 1
     for m in range(-1, PAIRS):
-        made = KNOTS * last_chunk + (2 if m < 0 else 2 * m + 7)
+        made = KNOTS * last_chunk + (3 if m < 0 else 2 * m + 7)
         begin = max(made + 1, free_step)
         products.append((begin, last_tile, max(0, 1 + 2 * m), 2 + 2 * m, (0, F_TILES)))
         free_step = begin + 1
@@ -156,6 +156,11 @@ def tile_kanblock_pa_kernel(tc, x, grid, w1_base, w1_spline, out):
         make_identity(nc, ident_f32[:])
         ident_bf = const.tile([P, P], BF16)
         make_identity(nc, ident_bf[:])
+
+        zero = const.tile([P, 1], F32)
+        nc.gpsimd.memset(zero[:], 0.0)
+        silu_of_zero = const.tile([P, 1], F32)
+        nc.scalar.activation(out=silu_of_zero[:], in_=zero[:], func=ACT.Silu)
 
         x_t = const.tile([P, TOKENS * PACK], BF16)
         a_codes = keep.tile([P, TOKENS * PASSES], U32, align_bytes=64)
@@ -194,12 +199,15 @@ def tile_kanblock_pa_kernel(tc, x, grid, w1_base, w1_spline, out):
                     nc.tensor.transpose(
                         turned[:, f, :], x_sb[:, nt, f * P : (f + 1) * P], ident_bf[:]
                     )
-                nc.vector.tensor_scalar(
-                    out=by_token(chunk_x(c))[:, :, i * P : (i + 1) * P, :],
-                    in0=turned[:].rearrange("p (h u) n -> p h n u", u=2),
-                    scalar1=knots[:, 0:1], scalar2=knots[:, KNOTS - 1 : KNOTS],
-                    op0=ALU.max, op1=ALU.min,
-                )
+                for h in [slice(0, 1), slice(1, 2)] if c == 0 else [slice(0, 2)]:
+                    nc.vector.tensor_scalar(
+                        out=by_token(chunk_x(c))[:, h, i * P : (i + 1) * P, :],
+                        in0=turned[:, 2 * h.start : 2 * h.stop, :].rearrange(
+                            "p (h u) n -> p h n u", u=2
+                        ),
+                        scalar1=knots[:, 0:1], scalar2=knots[:, KNOTS - 1 : KNOTS],
+                        op0=ALU.max, op1=ALU.min,
+                    )
 
         def silu_stage(c):
             silu = stage.tile([P, CHUNKS[c] * P, PACK], BF16, align_bytes=64, name="silu", bufs=1)
@@ -224,23 +232,20 @@ def tile_kanblock_pa_kernel(tc, x, grid, w1_base, w1_spline, out):
                 in_=live["silu", c][:].rearrange("p n t -> p (n t)"),
             )
 
-        def token_parts(step):
+        def parts_of(step):
+            width = width_of(step // KNOTS)
             if step > 0:
-                return [lambda plane: plane]
-            columns = 2 * P
-            return [
-                lambda plane, i=i: plane.rearrange("p (h r) -> p h r", h=2)[
-                    :, :, i * columns : (i + 1) * columns
-                ]
-                for i in range(CHUNKS[0])
-            ]
+                return [slice(0, width)]
+            piece = 2 * P
+            pieces = [h * CHUNKS[0] + i for i in range(CHUNKS[0]) for h in range(2)]
+            return [slice(n * piece, (n + 1) * piece) for n in pieces]
 
         def square_stage(step):
             c, j = divmod(step, KNOTS)
-            square = planes.tile([P, width_of(c)], F32, bufs=2)
-            for part in token_parts(step):
+            square = planes.tile([P, width_of(c)], F32)
+            for part in parts_of(step):
                 nc.scalar.activation(
-                    out=part(square[:]), in_=part(chunk_x(c)), func=ACT.Square,
+                    out=square[:, part], in_=chunk_x(c)[:, part], func=ACT.Square,
                     bias=knots[:, j : j + 1], scale=-1.0,
                 )
             live["square", step] = square
@@ -248,10 +253,10 @@ def tile_kanblock_pa_kernel(tc, x, grid, w1_base, w1_spline, out):
         def cube_stage(step):
             c, j = divmod(step, KNOTS)
             cube = planes.tile([P, width_of(c)], F32)
-            for part in token_parts(step):
+            for part in parts_of(step):
                 nc.vector.scalar_tensor_tensor(
-                    out=part(cube[:]), in0=part(chunk_x(c)), scalar=knots[:, j : j + 1],
-                    in1=part(live["square", step][:]), op0=ALU.subtract, op1=ALU.mult,
+                    out=cube[:, part], in0=chunk_x(c)[:, part], scalar=knots[:, j : j + 1],
+                    in1=live["square", step][:, part], op0=ALU.subtract, op1=ALU.mult,
                 )
             live["cube", step] = cube
 
@@ -259,7 +264,7 @@ def tile_kanblock_pa_kernel(tc, x, grid, w1_base, w1_spline, out):
             c, j = divmod(step, KNOTS)
             cube = live["cube", step]
             if 1 <= j <= NB:
-                above = planes.tile([P, width_of(c)], F32, bufs=2)
+                above = planes.tile([P, width_of(c)], F32)
                 nc.scalar.activation(
                     out=above[:], in_=cube[:], func=ACT.Relu, scale=rise_inner[:, j - 1 : j]
                 )
@@ -406,8 +411,9 @@ def tile_kanblock_pa_kernel(tc, x, grid, w1_base, w1_spline, out):
 
         with tc.manual_schedule(engines={mybir.EngineType.DVE}):
             turn_stage(0)
+            square_stage(0)
+            cube_stage(0)
             rise, rise_inner, neg_fall, neg_fall_inner = spline_factors(nc, const, knots)
-        square_stage(0)
         tail_step = KNOTS * last_chunk + KNOTS - 3
         for step in range(last_step + 1):
             c, j = divmod(step, KNOTS)
@@ -419,8 +425,9 @@ def tile_kanblock_pa_kernel(tc, x, grid, w1_base, w1_spline, out):
                 square_stage(step + 1)
             if step > tail_step and step <= n_steps:
                 side_stage(step - 1)
-            if step < n_steps:
+            if 0 < step < n_steps:
                 cube_stage(step)
+                inner_stage(step)
             made = [divmod(step - (1 if step > tail_step else 2) - (2 * m + 5), KNOTS)
                     for m in range(PAIRS)]
             joins = [(made_c, m) for m, (made_c, rest) in enumerate(made)
@@ -430,9 +437,9 @@ def tile_kanblock_pa_kernel(tc, x, grid, w1_base, w1_spline, out):
                 if made_c == last_chunk and (made_c, m) != last_pair:
                     bases_quantise_stage(made_c, m, slice(0, 2))
             if step < n_steps:
-                if j == 0:
-                    silu_stage(c)
                 if j == 1:
+                    silu_stage(c)
+                if j == 2:
                     silu_quantise_stage(c)
             for kind, ft, half, h, m in banks_of(step):
                 weight_bank_stage(kind, ft, half, h, m)
@@ -452,5 +459,3 @@ def tile_kanblock_pa_kernel(tc, x, grid, w1_base, w1_spline, out):
             for made_c, m in joins:
                 if made_c != last_chunk:
                     bases_quantise_stage(made_c, m, slice(0, 2))
-            if step < n_steps:
-                inner_stage(step)

@@ -29,10 +29,10 @@ ROWS_PER_F_TILE = F_TILE // P
 ROWS_PER_BANK = 2
 HALF = D // 2
 
-CHUNKS = (2, 1, 1)
+CHUNKS = (1, 1, 1, 1)
 VECTOR_BELOW = 4
 FIRST_BANK_BEAT = 2
-BANKS_PER_RUN = 12
+BANKS_PER_RUN = 10
 BEATS_PER_RUN = 5
 FLOPS = 2 * TOKENS * F_OUT * K_ALL
 
@@ -143,9 +143,9 @@ def tile_kanblock_pa_kernel(tc, x, grid, w1_base, w1_spline, out):
     with ExitStack() as pools:
         const = pools.enter_context(tc.tile_pool(name="const", bufs=1))
         keep = pools.enter_context(tc.tile_pool(name="keep", bufs=1))
-        loads = pools.enter_context(tc.tile_pool(name="loads", bufs=4))
-        stage = pools.enter_context(tc.tile_pool(name="stage", bufs=2))
-        planes = pools.enter_context(tc.tile_pool(name="planes", bufs=3))
+        loads = pools.enter_context(tc.tile_pool(name="loads", bufs=5))
+        stage = pools.enter_context(tc.tile_pool(name="stage", bufs=3))
+        planes = pools.enter_context(tc.tile_pool(name="planes", bufs=5))
         psum = pools.enter_context(tc.psum_pool(name="psum", bufs=8))
 
         x_sb = const.tile([P, TOKEN_TILES, D], BF16)
@@ -272,7 +272,7 @@ def tile_kanblock_pa_kernel(tc, x, grid, w1_base, w1_spline, out):
             if 3 <= j <= NB + 2:
                 below = planes.tile([P, width_of(c)], F32)
                 factor = neg_fall_inner[:, j - 3 : j - 2]
-                if c == 0 and j < VECTOR_BELOW:
+                if c < 2 and j < VECTOR_BELOW:
                     nc.vector.tensor_scalar(
                         out=below[:], in0=cube[:], scalar1=0.0, scalar2=factor,
                         op0=ALU.min, op1=ALU.mult,
@@ -296,7 +296,7 @@ def tile_kanblock_pa_kernel(tc, x, grid, w1_base, w1_spline, out):
             if j >= 4:
                 b = j - 4
                 if b % 2 == 0:
-                    right = planes.tile([P, 2, width_of(c)], BF16, bufs=2)
+                    right = planes.tile([P, 2, width_of(c)], BF16)
                     live["right", c, b // 2] = right
                 nc.vector.scalar_tensor_tensor(
                     out=live["right", c, b // 2][:, b % 2, :], in0=live["cube", step][:],
@@ -344,7 +344,7 @@ def tile_kanblock_pa_kernel(tc, x, grid, w1_base, w1_spline, out):
             g = 0 if kind == "base" else 1 + 2 * m + h
             if half == 0:
                 live["w_grouped", ft, g] = stage.tile(
-                    [P, F_TILE, PACK], BF16, align_bytes=64, name="w_grouped", tag="wide", bufs=4
+                    [P, F_TILE, PACK], BF16, align_bytes=64, name="w_grouped", tag="wide", bufs=5
                 )
             flipped = psum.tile([P, 2, ROWS_PER_BANK * P], F32, tag="bank")
             for a in range(ROWS_PER_BANK):
@@ -398,7 +398,7 @@ def tile_kanblock_pa_kernel(tc, x, grid, w1_base, w1_spline, out):
             for ft in range(fts[0], fts[1]):
                 cols = slice(ft * F_TILE, (ft + 1) * F_TILE)
                 result = stage.tile(
-                    [P, F_TILE], F32, align_bytes=64, name="result", tag="wide", bufs=4
+                    [P, F_TILE], F32, align_bytes=64, name="result", tag="wide", bufs=5
                 )
                 if ft % 2 == 0 or nt < last_tile:
                     nc.scalar.copy(out=result[:], in_=live["acc", nt, ft][:])
@@ -427,7 +427,6 @@ def tile_kanblock_pa_kernel(tc, x, grid, w1_base, w1_spline, out):
                 side_stage(step - 1)
             if 0 < step < n_steps:
                 cube_stage(step)
-                inner_stage(step)
             made = [divmod(step - (1 if step > tail_step else 2) - (2 * m + 5), KNOTS)
                     for m in range(PAIRS)]
             joins = [(made_c, m) for m, (made_c, rest) in enumerate(made)
@@ -459,3 +458,5 @@ def tile_kanblock_pa_kernel(tc, x, grid, w1_base, w1_spline, out):
             for made_c, m in joins:
                 if made_c != last_chunk:
                     bases_quantise_stage(made_c, m, slice(0, 2))
+            if step < n_steps:
+                inner_stage(step)

from contextlib import ExitStack

import concourse.mybir as mybir
from concourse.masks import make_identity

F32 = mybir.dt.float32
BF16 = mybir.dt.bfloat16
U32 = mybir.dt.uint32
U8 = mybir.dt.uint8
FP8X4 = mybir.dt.float8_e4m3fn_x4
ALU = mybir.AluOpType
ACT = mybir.ActivationFunctionType

P = 128
PACK = 4
K_PASS = P * PACK
TOKENS = 512
D = 512
F_OUT = 2048
KNOTS = 12
NB = 8
PAIRS = NB // 2
K_ALL = D + D * NB
PASSES = K_ALL // K_PASS
TOKEN_TILES = TOKENS // P
F_TILE = 512
F_TILES = F_OUT // F_TILE
ROWS_PER_F_TILE = F_TILE // P
ROWS_PER_BANK = 2
HALF = D // 2

CHUNKS = (1, 1, 1, 1)
VECTOR_BELOW = 4
FIRST_BANK_BEAT = 2
BANKS_PER_RUN = 10
BEATS_PER_RUN = 5
FLOPS = 2 * TOKENS * F_OUT * K_ALL


def spline_knots(nc, const, grid):
    knots_bf = const.tile([P, KNOTS], BF16)
    nc.scalar.dma_start(out=knots_bf[:], in_=grid.partition_broadcast(P))
    knots = const.tile([P, KNOTS], F32)
    nc.vector.tensor_copy(out=knots[:], in_=knots_bf[:])
    return knots


def spline_factors(nc, const, knots):
    n_cubes = KNOTS - 3
    fall_at = n_cubes
    gap1_at = 2 * n_cubes
    den = const.tile([P, gap1_at + KNOTS - 1], F32)
    gap1 = den[:, gap1_at:]
    nc.gpsimd.tensor_sub(out=gap1, in0=knots[:, 1:], in1=knots[:, : KNOTS - 1])
    gap2 = const.tile([P, KNOTS - 2], F32)
    nc.gpsimd.tensor_sub(out=gap2[:], in0=knots[:, 2:], in1=knots[:, : KNOTS - 2])
    gap3 = const.tile([P, KNOTS - 3], F32)
    nc.gpsimd.tensor_sub(out=gap3[:], in0=knots[:, 3:], in1=knots[:, : KNOTS - 3])
    neg_gap3 = const.tile([P, KNOTS - 3], F32)
    nc.gpsimd.tensor_sub(out=neg_gap3[:], in0=knots[:, : KNOTS - 3], in1=knots[:, 3:])
    gap4 = const.tile([P, KNOTS - 4], F32)
    nc.gpsimd.tensor_sub(out=gap4[:], in0=knots[:, 4:], in1=knots[:, : KNOTS - 4])

    rise_pair = const.tile([P, n_cubes], F32)
    nc.gpsimd.tensor_mul(out=rise_pair[:], in0=den[:, gap1_at : gap1_at + n_cubes], in1=gap2[:, :n_cubes])
    nc.gpsimd.tensor_mul(out=den[:, :fall_at], in0=rise_pair[:], in1=gap3[:])
    fall_pair = const.tile([P, n_cubes], F32)
    nc.gpsimd.tensor_mul(out=fall_pair[:], in0=den[:, gap1_at + 2 :], in1=gap2[:, 1:])
    nc.gpsimd.tensor_mul(out=den[:, fall_at:gap1_at], in0=fall_pair[:], in1=neg_gap3[:])
    inverse = const.tile([P, gap1_at + KNOTS - 1], F32)
    nc.vector.reciprocal(out=inverse[:], in_=den[:])
    rise = inverse[:, :fall_at]
    neg_fall = inverse[:, fall_at:gap1_at]

    rise_ratio = const.tile([P, NB], F32)
    nc.gpsimd.tensor_mul(out=rise_ratio[:], in0=gap4[:], in1=inverse[:, gap1_at : gap1_at + NB])
    rise_inner = const.tile([P, NB], F32)
    nc.gpsimd.tensor_mul(out=rise_inner[:], in0=rise_ratio[:], in1=inverse[:, 1:fall_at])
    fall_ratio = const.tile([P, NB], F32)
    nc.gpsimd.tensor_mul(out=fall_ratio[:], in0=gap4[:], in1=inverse[:, gap1_at + 3 :])
    neg_fall_inner = const.tile([P, NB], F32)
    nc.gpsimd.tensor_mul(
        out=neg_fall_inner[:], in0=fall_ratio[:], in1=inverse[:, fall_at : fall_at + NB]
    )
    return rise, rise_inner, neg_fall, neg_fall_inner


def tile_kanblock_pa_kernel(tc, x, grid, w1_base, w1_spline, out):
    nc = tc.nc
    x_rows = x.rearrange("b s d -> (b s) d").rearrange("(t p) d -> p t d", p=P)
    base_rows = w1_base.rearrange("(a p) k -> p a k", p=P)
    spline_rows = w1_spline.rearrange("(a p) i b -> p a (i b)", p=P)

    n_steps = KNOTS * len(CHUNKS)
    first_tile = [sum(CHUNKS[:c]) for c in range(len(CHUNKS))]
    last_tile = TOKEN_TILES - 1
    last_chunk = len(CHUNKS) - 1
    last_pair = (last_chunk, PAIRS - 1)

    banks = []
    for ft in range(F_TILES):
        for half in range(2):
            banks.append(("base", ft, half, 0, 0))
        for h in range(2):
            for m in range(PAIRS):
                for half in range(2):
                    banks.append(("spline", ft, half, h, m))
    step_of_beat = []
    for c, tiles in enumerate(CHUNKS):
        for j in range(KNOTS):
            step_of_beat += tiles * [KNOTS * c + j]

    def bank_step(i):
        return step_of_beat[FIRST_BANK_BEAT + i * BEATS_PER_RUN // BANKS_PER_RUN]

    weights_done = [
        bank_step((ft + 1) * len(banks) // F_TILES - 1) + 1 for ft in range(F_TILES)
    ]

    ready = []
    for c in range(last_chunk):
        for nt in range(first_tile[c], first_tile[c] + CHUNKS[c]):
            for ft in range(F_TILES):
                made = KNOTS * c + 2 * PAIRS + 5
                ready.append((max(made, weights_done[ft]) + 1, nt, ft))
    products = []
    free_step = 0
    for begin, nt, ft in sorted(ready):
        begin = max(begin, free_step)
        if begin <= weights_done[F_TILES - 1]:
            products.append((begin, nt, 0, PASSES // 2 - 1, (ft, ft + 1)))
            products.append((begin + 1, nt, PASSES // 2, PASSES - 1, (ft, ft + 1)))
        else:
            products.append((begin, nt, 0, PASSES - 1, (ft, ft + 1)))
        free_step = products[-1][0] + 1
    for m in range(-1, PAIRS):
        made = KNOTS * last_chunk + (3 if m < 0 else 2 * m + 7)
        begin = max(made + 1, free_step)
        products.append((begin, last_tile, max(0, 1 + 2 * m), 2 + 2 * m, (0, F_TILES)))
        free_step = begin + 1
    last_step = products[-1][0] + 1

    with ExitStack() as pools:
        const = pools.enter_context(tc.tile_pool(name="const", bufs=1))
        keep = pools.enter_context(tc.tile_pool(name="keep", bufs=1))
        loads = pools.enter_context(tc.tile_pool(name="loads", bufs=5))
        stage = pools.enter_context(tc.tile_pool(name="stage", bufs=3))
        planes = pools.enter_context(tc.tile_pool(name="planes", bufs=5))
        psum = pools.enter_context(tc.psum_pool(name="psum", bufs=8))

        x_sb = const.tile([P, TOKEN_TILES, D], BF16)
        for nt in range(CHUNKS[0]):
            nc.sync.dma_start(out=x_sb[:, nt, :], in_=x_rows[:, nt, :])
        knots = spline_knots(nc, const, grid)
        ident_f32 = const.tile([P, P], F32)
        make_identity(nc, ident_f32[:])
        ident_bf = const.tile([P, P], BF16)
        make_identity(nc, ident_bf[:])

        zero = const.tile([P, 1], F32)
        nc.gpsimd.memset(zero[:], 0.0)
        silu_of_zero = const.tile([P, 1], F32)
        nc.scalar.activation(out=silu_of_zero[:], in_=zero[:], func=ACT.Silu)

        x_t = const.tile([P, TOKENS * PACK], BF16)
        a_codes = keep.tile([P, TOKENS * PASSES], U32, align_bytes=64)
        a_scales = keep.tile([P, TOKENS * PASSES], U8, align_bytes=64)
        w_codes = keep.tile([P, PASSES, F_OUT], U32, align_bytes=64)
        w_scales = keep.tile([P, (PASSES + 3) // 4, F_OUT], U8, align_bytes=64)

        live = {}

        def chunk_tokens(c):
            return slice(first_tile[c] * P, (first_tile[c] + CHUNKS[c]) * P)

        def width_of(c):
            return PACK * P * CHUNKS[c]

        def chunk_x(c):
            tokens = chunk_tokens(c)
            return x_t[:, PACK * tokens.start : PACK * tokens.stop]

        def by_token(plane):
            return plane.rearrange("p (h n u) -> p h n u", h=2, u=2)

        def of_passes(tile, c):
            tokens = chunk_tokens(c)
            part = tile[:, PASSES * tokens.start : PASSES * tokens.stop]
            return part.rearrange("p (g n) -> p g n", g=PASSES)

        def w_scale_rows(g, cols):
            return w_scales[4 * (g % 4) :, g // 4, cols]

        def turn_stage(c):
            for i in range(CHUNKS[c]):
                nt = first_tile[c] + i
                turned = psum.tile([P, PACK, P], BF16, tag="bank")
                for f in range(PACK):
                    nc.tensor.transpose(
                        turned[:, f, :], x_sb[:, nt, f * P : (f + 1) * P], ident_bf[:]
                    )
                for h in [slice(0, 1), slice(1, 2)] if c == 0 else [slice(0, 2)]:
                    nc.vector.tensor_scalar(
                        out=by_token(chunk_x(c))[:, h, i * P : (i + 1) * P, :],
                        in0=turned[:, 2 * h.start : 2 * h.stop, :].rearrange(
                            "p (h u) n -> p h n u", u=2
                        ),
                        scalar1=knots[:, 0:1], scalar2=knots[:, KNOTS - 1 : KNOTS],
                        op0=ALU.max, op1=ALU.min,
                    )

        def silu_stage(c):
            silu = stage.tile([P, CHUNKS[c] * P, PACK], BF16, align_bytes=64, name="silu", bufs=1)
            for i in range(CHUNKS[c]):
                words = x_sb[:, first_tile[c] + i, :].bitcast(F32)
                turned = psum.tile([P, 2, P], F32, tag="bank")
                for u in range(2):
                    nc.tensor.transpose(
                        turned[:, u, :], words[:, u * P : (u + 1) * P], ident_f32[:]
                    )
                nc.scalar.activation(
                    out=silu[:, i * P : (i + 1) * P, :].rearrange("p n (u e) -> p n u e", u=2),
                    in_=turned[:].bitcast(BF16).rearrange("p u (n e) -> p n u e", e=2),
                    func=ACT.Silu,
                )
            live["silu", c] = silu

        def silu_quantise_stage(c):
            nc.vector.quantize_mx(
                out=of_passes(a_codes, c)[:, 0, :].bitcast(FP8X4),
                scales=of_passes(a_scales, c)[:, 0, :],
                in_=live["silu", c][:].rearrange("p n t -> p (n t)"),
            )

        def parts_of(step):
            width = width_of(step // KNOTS)
            if step > 0:
                return [slice(0, width)]
            piece = 2 * P
            pieces = [h * CHUNKS[0] + i for i in range(CHUNKS[0]) for h in range(2)]
            return [slice(n * piece, (n + 1) * piece) for n in pieces]

        def square_stage(step):
            c, j = divmod(step, KNOTS)
            square = planes.tile([P, width_of(c)], F32)
            for part in parts_of(step):
                nc.scalar.activation(
                    out=square[:, part], in_=chunk_x(c)[:, part], func=ACT.Square,
                    bias=knots[:, j : j + 1], scale=-1.0,
                )
            live["square", step] = square

        def cube_stage(step):
            c, j = divmod(step, KNOTS)
            cube = planes.tile([P, width_of(c)], F32)
            for part in parts_of(step):
                nc.vector.scalar_tensor_tensor(
                    out=cube[:, part], in0=chunk_x(c)[:, part], scalar=knots[:, j : j + 1],
                    in1=live["square", step][:, part], op0=ALU.subtract, op1=ALU.mult,
                )
            live["cube", step] = cube

        def inner_stage(step):
            c, j = divmod(step, KNOTS)
            cube = live["cube", step]
            if 1 <= j <= NB:
                above = planes.tile([P, width_of(c)], F32)
                nc.scalar.activation(
                    out=above[:], in_=cube[:], func=ACT.Relu, scale=rise_inner[:, j - 1 : j]
                )
                live["above", step] = above
            if 3 <= j <= NB + 2:
                below = planes.tile([P, width_of(c)], F32)
                factor = neg_fall_inner[:, j - 3 : j - 2]
                if c < 2 and j < VECTOR_BELOW:
                    nc.vector.tensor_scalar(
                        out=below[:], in0=cube[:], scalar1=0.0, scalar2=factor,
                        op0=ALU.min, op1=ALU.mult,
                    )
                else:
                    nc.scalar.activation(out=below[:], in_=cube[:], func=ACT.Relu, scale=factor)
                live["below", step] = below

        def side_stage(step):
            c, j = divmod(step, KNOTS)
            if 1 <= j <= NB:
                b = j - 1
                if b % 2 == 0:
                    left = planes.tile([P, 2, width_of(c)], BF16)
                    live["left", c, b // 2] = left
                nc.vector.scalar_tensor_tensor(
                    out=live["left", c, b // 2][:, b % 2, :], in0=live["cube", step - 1][:],
                    scalar=rise[:, b : b + 1], in1=live["above", step][:],
                    op0=ALU.mult, op1=ALU.subtract,
                )
            if j >= 4:
                b = j - 4
                if b % 2 == 0:
                    right = planes.tile([P, 2, width_of(c)], BF16)
                    live["right", c, b // 2] = right
                nc.vector.scalar_tensor_tensor(
                    out=live["right", c, b // 2][:, b % 2, :], in0=live["cube", step][:],
                    scalar=neg_fall[:, b + 1 : b + 2], in1=live["below", step - 1][:],
                    op0=ALU.mult, op1=ALU.subtract,
                )

        def join_stage(c, m):
            bases = stage.tile([P, width_of(c), 2], BF16, align_bytes=64, name="bases")
            live["bases", c, m] = bases
            parts = 1
            if (c, m) == last_pair:
                parts = 2
            for part in range(parts):
                qs = slice(part * width_of(c) // parts, (part + 1) * width_of(c) // parts)
                nc.vector.scalar_tensor_tensor(
                    out=bases[:, qs, :],
                    in0=live["left", c, m][:, :, qs].rearrange("p e q -> p q e"), scalar=0.0,
                    in1=live["right", c, m][:, :, qs].rearrange("p e q -> p q e"),
                    op0=ALU.max, op1=ALU.max,
                )
                if (c, m) == last_pair:
                    bases_quantise_stage(c, m, slice(part, part + 1))

        def bases_quantise_stage(c, m, h):
            qs = slice(h.start * width_of(c) // 2, h.stop * width_of(c) // 2)
            passes = slice(1 + 2 * m + h.start, 1 + 2 * m + h.stop)
            nc.vector.quantize_mx(
                out=of_passes(a_codes, c)[:, passes, :].rearrange("p g n -> p (g n)").bitcast(FP8X4),
                scales=of_passes(a_scales, c)[:, passes, :].rearrange("p g n -> p (g n)"),
                in_=live["bases", c, m][:, qs, :].rearrange("p q e -> p (q e)"),
            )

        def weight_bank_stage(kind, ft, half, h, m):
            first_row = ft * ROWS_PER_F_TILE + half * ROWS_PER_BANK
            rows = slice(first_row, first_row + ROWS_PER_BANK)
            if m == 0:
                raw = loads.tile([P, ROWS_PER_BANK, HALF * NB], BF16, tag="w_raw")
                if kind == "base":
                    nc.sync.dma_start(out=raw[:, :, :D], in_=base_rows[:, rows, :])
                else:
                    cols = slice(h * HALF * NB, (h + 1) * HALF * NB)
                    nc.sync.dma_start(out=raw[:], in_=spline_rows[:, rows, cols])
                live["w_words", half] = raw[:].bitcast(F32)
            g = 0 if kind == "base" else 1 + 2 * m + h
            if half == 0:
                live["w_grouped", ft, g] = stage.tile(
                    [P, F_TILE, PACK], BF16, align_bytes=64, name="w_grouped", tag="wide", bufs=5
                )
            flipped = psum.tile([P, 2, ROWS_PER_BANK * P], F32, tag="bank")
            for a in range(ROWS_PER_BANK):
                for u in range(2):
                    if kind == "base":
                        words = slice(u * P, (u + 1) * P)
                    else:
                        words = slice(PAIRS * P * u + m, PAIRS * P * (u + 1), PAIRS)
                    nc.tensor.transpose(
                        flipped[:, u, a * P : (a + 1) * P], live["w_words", half][:, a, words],
                        ident_f32[:],
                    )
            first_col = half * ROWS_PER_BANK * P
            nc.scalar.copy(
                out=live["w_grouped", ft, g][
                    :, first_col : first_col + ROWS_PER_BANK * P, :
                ].bitcast(F32),
                in_=flipped[:].rearrange("p u f -> p f u"),
            )

        def weight_quantise_stage(ft, g):
            cols = slice(ft * F_TILE, (ft + 1) * F_TILE)
            nc.vector.quantize_mx(
                out=w_codes[:, g, cols].bitcast(FP8X4),
                scales=w_scale_rows(g, cols),
                in_=live["w_grouped", ft, g][:].rearrange("p f t -> p (f t)"),
            )

        def multiply_stage(nt, first, last, fts):
            order = [(ft, g) for ft in range(fts[0], fts[1]) for g in range(first, last + 1)]
            if nt == last_tile:
                order = [(ft, g) for g in range(first, last + 1) for ft in range(fts[0], fts[1])]
            c = max(c for c in range(len(CHUNKS)) if first_tile[c] <= nt)
            tokens = slice((nt - first_tile[c]) * P, (nt - first_tile[c] + 1) * P)
            for ft, g in order:
                if g == 0:
                    acc = psum.tile([P, F_TILE], F32, tag="bank")
                    live["acc", nt, ft] = acc
                cols = slice(ft * F_TILE, (ft + 1) * F_TILE)
                nc.tensor.matmul_mx(
                    out=live["acc", nt, ft][:],
                    lhsT=of_passes(a_codes, c)[:, g, tokens].bitcast(FP8X4),
                    lhsT_scale=of_passes(a_scales, c)[:, g, tokens],
                    rhs=w_codes[:, g, cols].bitcast(FP8X4),
                    rhs_scale=w_scale_rows(g, cols),
                    start=(g == 0),
                    stop=(g == PASSES - 1),
                )

        def store_stage(nt, fts):
            for ft in range(fts[0], fts[1]):
                cols = slice(ft * F_TILE, (ft + 1) * F_TILE)
                result = stage.tile(
                    [P, F_TILE], F32, align_bytes=64, name="result", tag="wide", bufs=5
                )
                if ft % 2 == 0 or nt < last_tile:
                    nc.scalar.copy(out=result[:], in_=live["acc", nt, ft][:])
                else:
                    nc.vector.tensor_copy(out=result[:], in_=live["acc", nt, ft][:])
                nc.sync.dma_start(out=out[nt * P : (nt + 1) * P, cols], in_=result[:])

        def banks_of(step):
            return [bank for i, bank in enumerate(banks) if bank_step(i) == step]

        with tc.manual_schedule(engines={mybir.EngineType.DVE}):
            turn_stage(0)
            square_stage(0)
            cube_stage(0)
            rise, rise_inner, neg_fall, neg_fall_inner = spline_factors(nc, const, knots)
        tail_step = KNOTS * last_chunk + KNOTS - 3
        for step in range(last_step + 1):
            c, j = divmod(step, KNOTS)
            if step == tail_step:
                pools.enter_context(tc.manual_schedule(engines={mybir.EngineType.DVE}))
            if step + 1 < n_steps:
                if (step + 1) % KNOTS == 0:
                    turn_stage(c + 1)
                square_stage(step + 1)
            if step > tail_step and step <= n_steps:
                side_stage(step - 1)
            if 0 < step < n_steps:
                cube_stage(step)
            made = [divmod(step - (1 if step > tail_step else 2) - (2 * m + 5), KNOTS)
                    for m in range(PAIRS)]
            joins = [(made_c, m) for m, (made_c, rest) in enumerate(made)
                     if rest == 0 and 0 <= made_c < len(CHUNKS)]
            for made_c, m in joins:
                join_stage(made_c, m)
                if made_c == last_chunk and (made_c, m) != last_pair:
                    bases_quantise_stage(made_c, m, slice(0, 2))
            if step < n_steps:
                if j == 1:
                    silu_stage(c)
                if j == 2:
                    silu_quantise_stage(c)
            for kind, ft, half, h, m in banks_of(step):
                weight_bank_stage(kind, ft, half, h, m)
            if step == 0:
                for later in range(CHUNKS[0], TOKEN_TILES):
                    nc.sync.dma_start(out=x_sb[:, later, :], in_=x_rows[:, later, :])
            for kind, ft, half, h, m in banks_of(step - 1):
                if half == 1:
                    weight_quantise_stage(ft, 0 if kind == "base" else 1 + 2 * m + h)
            for begin, of_tile, first, last, fts in products:
                if begin == step:
                    multiply_stage(of_tile, first, last, fts)
                if begin == step - 1 and last == PASSES - 1:
                    store_stage(of_tile, fts)
            if 1 <= step <= tail_step:
                side_stage(step - 1)
            for made_c, m in joins:
                if made_c != last_chunk:
                    bases_quantise_stage(made_c, m, slice(0, 2))
            if step < n_steps:
                inner_stage(step)
